import numpy as np
import ml_dtypes

BF16 = ml_dtypes.bfloat16


def bf(x):
    return np.asarray(x, np.float32).astype(BF16)


def f32(x):
    return np.asarray(x, np.float32)


def f64(x):
    return np.asarray(x).astype(np.float64)


def striped(idx):
    return np.tile(idx.reshape(-1, 16).T, (8, 1))


B, S, K, FI, FO, C, N, H, R = 2, 1024, 4, 512, 512, 1024, 4096, 512, 8
EPS = 1e-5
LIM = np.sqrt(2.0) * np.sqrt(6.0 / (FI + FO))


def setup_inputs():
    x = f32(np.random.standard_normal((C, S)))
    w_self = bf(np.random.uniform(-LIM, LIM, (FI, FO)))
    bias_self = f32(0.1 * np.random.standard_normal((FO, 1)))
    w_nei = bf(np.random.uniform(-LIM, LIM, (FI, FO)))
    bias_nei = f32(0.1 * np.random.standard_normal((FO, 1)))
    gamma = f32(1.0 + 0.1 * np.random.standard_normal((FO + FO, 1)))
    beta = f32(0.1 * np.random.standard_normal((FO + FO, 1)))
    idx = np.concatenate([np.random.permutation(S)[:H] for _ in range(R)])
    return {"x": x, "w_self": w_self, "bias_self": bias_self, "w_nei": w_nei, "bias_nei": bias_nei, "gamma": gamma, "beta": beta, "offs": striped(idx)}


def reference(x, w_self, bias_self, w_nei, bias_nei, gamma, beta, offs):
    idx = offs[:16].T.reshape(-1)
    xs = f64(x)
    agg = xs[:, idx].reshape(C, K, S).sum(axis=1) / K
    h_self = f64(w_self).T @ xs.reshape(B, FI, S) + f64(bias_self)
    h_nei = f64(w_nei).T @ agg.reshape(B, FI, S) + f64(bias_nei)
    h = np.concatenate([h_self, h_nei], axis=1)
    nrm = np.sqrt((h * h).sum(axis=1, keepdims=True))
    r = np.maximum(h / nrm, 0.0)
    mu = r.mean(axis=(0, 2), keepdims=True)
    var = ((r - mu) * (r - mu)).mean(axis=(0, 2), keepdims=True)
    y = (r - mu) / np.sqrt(var + EPS) * f64(gamma) + f64(beta)
    return y.reshape(B * (FO + FO), S)

@@ -1,0 +1,260 @@
+import concourse.mybir as mybir
+from concourse.masks import make_identity
+
+F32 = mybir.dt.float32
+BF16 = mybir.dt.bfloat16
+U16 = mybir.dt.uint16
+FUNC = mybir.ActivationFunctionType
+ALU = mybir.AluOpType
+
+P = 128
+GRAPHS = 2
+NODES = 1024
+NEIGHBOURS = 4
+F_IN = 512
+F_OUT = 512
+CHANNELS = 2 * F_OUT
+F_BLOCKS = F_IN // P
+Q_BLOCKS = CHANNELS // P
+NODE_BLOCKS = NODES // P
+HALF_BLOCKS = F_OUT // P
+WIDE = 512
+NARROW = 256
+GROUP = 2
+COUNT = GRAPHS * NODES
+EPS = 1e-5
+
+R_STEP = P + 2
+GRAMS_IN_BANK = 3
+GRAM_BANKS = 3
+
+FLOPS = 2 * GRAPHS * NODES * F_IN * CHANNELS
+
+
+def tile_batchedgraphsagemean1_b_kernel(
+    tc, x, w_self, bias_self, w_nei, bias_nei, gamma, beta, offs, out
+):
+    nc = tc.nc
+    with (
+        tc.tile_pool(name="held", bufs=1) as held,
+        tc.tile_pool(name="sums", bufs=3 * F_BLOCKS) as sums,
+        tc.tile_pool(name="means", bufs=2 * F_BLOCKS) as means,
+        tc.tile_pool(name="small", bufs=3 * GROUP) as small,
+        tc.tile_pool(name="scratch", bufs=2) as scratch,
+        tc.tile_pool(name="results", bufs=6) as results,
+        tc.psum_pool(name="gram_banks", bufs=1) as gram_banks,
+    ):
+        lists = held.tile([P, NEIGHBOURS * NODES // 16], U16, name="lists")
+        nc.sync.dma_start(lists[:], offs)
+        x_f32 = [held.tile([P, NODES], F32, name=f"x_f32_{i}") for i in range(GRAPHS * F_BLOCKS)]
+        for i in range(F_BLOCKS):
+            nc.sync.dma_start(x_f32[i][:], x[i * P : (i + 1) * P, :])
+        weights = {}
+        for part, w in (("self", w_self), ("nei", w_nei)):
+            weights[part] = held.tile([P, F_BLOCKS, F_OUT], BF16, name=f"w_{part}")
+            nc.sync.dma_start(weights[part][:], w.rearrange("(a p) q -> p a q", p=P))
+        for i in range(F_BLOCKS, GRAPHS * F_BLOCKS):
+            nc.sync.dma_start(x_f32[i][:], x[i * P : (i + 1) * P, :])
+
+        bias_f32 = held.tile([1, CHANNELS], F32, name="bias_f32")
+        nc.scalar.dma_start(bias_f32[:, 0:F_OUT], bias_self.rearrange("q o -> o q"))
+        nc.scalar.dma_start(bias_f32[:, F_OUT:CHANNELS], bias_nei.rearrange("q o -> o q"))
+        gamma_t = held.tile([P, Q_BLOCKS], F32, name="gamma_t")
+        beta_t = held.tile([P, Q_BLOCKS], F32, name="beta_t")
+        with nc.allow_non_contiguous_dma(reason="one 4-byte value to a partition, 8 KiB in all"):
+            nc.scalar.dma_start(gamma_t[:], gamma.rearrange("(j p) o -> p (j o)", p=P))
+            nc.scalar.dma_start(beta_t[:], beta.rearrange("(j p) o -> p (j o)", p=P))
+
+        zeros = held.tile([P, WIDE], F32, name="zeros")
+        nc.gpsimd.memset(zeros[:], 0.0)
+        eps_t = held.tile([P, 1], F32, name="eps_t")
+        nc.gpsimd.memset(eps_t[:], EPS)
+        ident_bf = held.tile([P, P], BF16, name="ident_bf")
+        make_identity(nc, ident_bf[:])
+        ident_f32 = held.tile([P, P], F32, name="ident_f32")
+        make_identity(nc, ident_f32[:])
+        first_row = held.tile([P, P], BF16, name="first_row")
+        nc.gpsimd.memset(first_row[:], 0.0)
+        nc.gpsimd.memset(first_row[0:1, :], 1.0)
+        bias_rows = held.tile([P, CHANNELS], BF16, name="bias_rows")
+        nc.gpsimd.memset(bias_rows[:], 0.0)
+        nc.scalar.copy(bias_rows[0:1, :], bias_f32[:])
+        r_tiles = [
+            [held.tile([P, Q_BLOCKS, R_STEP], BF16, name=f"r_{b}_{n}") for n in range(NODE_BLOCKS)]
+            for b in range(GRAPHS)
+        ]
+        for b in range(GRAPHS):
+            for n in range(NODE_BLOCKS):
+                nc.gpsimd.memset(r_tiles[b][n][:, :, P : P + 1], 1.0)
+
+        x_bf = [held.tile([P, NODES], BF16, name=f"x_bf_{i}") for i in range(GRAPHS * F_BLOCKS)]
+        for i in range(GRAPHS * F_BLOCKS):
+            nc.scalar.copy(x_bf[i][:], x_f32[i][:])
+
+        grams = [
+            gram_banks.tile([P, GRAMS_IN_BANK * R_STEP], F32, name=f"gram_{t}")
+            for t in range(GRAM_BANKS)
+        ]
+
+        pieces = [(0, c0, WIDE) for c0 in range(0, NODES, WIDE)]
+        pieces += [(1, c0, NARROW) for c0 in range(0, NODES, NARROW)]
+        blocks = [(b, n) for b, c0, width in pieces for n in range(c0 // P, (c0 + width) // P)]
+
+        with tc.psum_pool(name="h_banks", bufs=GROUP) as h_banks:
+
+            def project(part, half, nodes_of):
+                h_half = h_banks.tile([P, F_OUT], F32, name=f"h_{part}")
+                nc.tensor.matmul(
+                    h_half[:],
+                    lhsT=first_row[:],
+                    rhs=bias_rows[:, half * F_OUT : (half + 1) * F_OUT],
+                    start=True,
+                    stop=False,
+                )
+                for f in range(F_BLOCKS):
+                    nc.tensor.matmul(
+                        h_half[:],
+                        lhsT=nodes_of[f],
+                        rhs=weights[part][:, f, :],
+                        start=False,
+                        stop=(f == F_BLOCKS - 1),
+                    )
+                return h_half
+
+            def sum_of_squares(h_half, total):
+                squares = scratch.tile([P, F_OUT], BF16, name="squares")
+                nc.scalar.activation(squares[:], h_half[:], FUNC.Square, accum_out=total)
+
+            def begin(block):
+                b, n = block
+                h_self = project(
+                    "self", 0, [x_bf[b * F_BLOCKS + f][:, n * P : (n + 1) * P] for f in range(F_BLOCKS)]
+                )
+                square_sums = small.tile([P, 2], F32, name="square_sums")
+                sum_of_squares(h_self, square_sums[:, 0:1])
+                return h_self, square_sums
+
+            begun = {}
+            for block in blocks[0:GROUP]:
+                begun[block] = begin(block)
+
+            for b, c0, width in pieces:
+                running = [zeros[:, 0:width] for f in range(F_BLOCKS)]
+                for k in range(NEIGHBOURS):
+                    first = (k * NODES + c0) // 16
+                    piece = lists[:, first : first + width // 16]
+                    for f in range(F_BLOCKS):
+                        longer = sums.tile([P, width], F32, name="running_sum")
+                        nc.vector.tensor_tensor(
+                            longer[:], x_f32[b * F_BLOCKS + f][:].indirect(piece), running[f], ALU.add
+                        )
+                        running[f] = longer[:]
+                agg_bf = [means.tile([P, width], BF16, name="agg_bf") for f in range(F_BLOCKS)]
+                for f in range(F_BLOCKS):
+                    nc.scalar.activation(agg_bf[f][:], running[f], FUNC.Copy, scale=1.0 / NEIGHBOURS)
+
+                for n0 in range(c0 // P, (c0 + width) // P, GROUP):
+                    group = [(b, n) for n in range(n0, n0 + GROUP)]
+                    h_nei = {}
+                    for block in group:
+                        in_piece = slice(block[1] * P - c0, (block[1] + 1) * P - c0)
+                        h_nei[block] = project(
+                            "nei", 1, [agg_bf[f][:, in_piece] for f in range(F_BLOCKS)]
+                        )
+                    for block in group:
+                        h_self, square_sums = begun[block]
+                        sum_of_squares(h_nei[block], square_sums[:, 1:2])
+                        inv_norm = small.tile([P, 1], F32, name="inv_norm")
+                        nc.scalar.activation(
+                            inv_norm[:],
+                            square_sums[:, 0:1],
+                            FUNC.Abs_reciprocal_sqrt,
+                            bias=square_sums[:, 1:2],
+                        )
+                        r = r_tiles[block[0]][block[1]]
+                        for half, h_half in enumerate((h_self, h_nei[block])):
+                            nc.scalar.activation(
+                                r[:, half * HALF_BLOCKS : (half + 1) * HALF_BLOCKS, 0:P],
+                                h_half[:].rearrange("p (j c) -> p j c", c=P),
+                                FUNC.Relu,
+                                scale=inv_norm[:, 0:1],
+                            )
+                    for block in group:
+                        r = r_tiles[block[0]][block[1]]
+                        turn = blocks.index(block)
+                        for j in range(Q_BLOCKS):
+                            place = (j % GRAMS_IN_BANK) * R_STEP
+                            last_in_bank = j % GRAMS_IN_BANK == GRAMS_IN_BANK - 1 or j == Q_BLOCKS - 1
+                            nc.tensor.matmul(
+                                grams[j // GRAMS_IN_BANK][:, place : place + P + 1],
+                                lhsT=r[:, j, 0:P],
+                                rhs=r[:, j, 0 : P + 1],
+                                start=(turn == 0 and j % GRAMS_IN_BANK == 0),
+                                stop=(turn == len(blocks) - 1 and last_in_bank),
+                            )
+                        if turn + GROUP < len(blocks):
+                            begun[blocks[turn + GROUP]] = begin(blocks[turn + GROUP])
+
+        mean = held.tile([P, Q_BLOCKS], F32, name="mean")
+        mean_of_squares = held.tile([P, Q_BLOCKS], F32, name="mean_of_squares")
+        for t in range(GRAM_BANKS):
+            in_bank = min(GRAMS_IN_BANK, Q_BLOCKS - t * GRAMS_IN_BANK)
+            nc.scalar.activation(
+                mean[:, t * GRAMS_IN_BANK : t * GRAMS_IN_BANK + in_bank],
+                grams[t][:, P : P + (in_bank - 1) * R_STEP + 1 : R_STEP],
+                FUNC.Copy,
+                scale=1.0 / COUNT,
+            )
+        square_of_mean = held.tile([P, Q_BLOCKS], F32, name="square_of_mean")
+        nc.scalar.activation(square_of_mean[:], mean[:], FUNC.Square)
+        for j in range(Q_BLOCKS):
+            place = (j % GRAMS_IN_BANK) * R_STEP
+            diagonal = scratch.tile([P, P], F32, name="diagonal")
+            nc.vector.scalar_tensor_tensor(
+                out=diagonal[:],
+                in0=grams[j // GRAMS_IN_BANK][:, place : place + P],
+                scalar=1.0 / COUNT,
+                in1=ident_f32[:],
+                op0=ALU.mult,
+                op1=ALU.mult,
+                accum_out=mean_of_squares[:, j : j + 1],
+            )
+        variance = held.tile([P, Q_BLOCKS], F32, name="variance")
+        nc.vector.tensor_tensor(variance[:], mean_of_squares[:], square_of_mean[:], ALU.subtract)
+        inv_std = held.tile([P, Q_BLOCKS], F32, name="inv_std")
+        nc.scalar.activation(inv_std[:], variance[:], FUNC.Abs_reciprocal_sqrt, bias=eps_t[:, 0:1])
+        gain = held.tile([P, Q_BLOCKS], F32, name="gain")
+        nc.vector.tensor_tensor(gain[:], gamma_t[:], inv_std[:], ALU.mult)
+        mean_gain = held.tile([P, Q_BLOCKS], F32, name="mean_gain")
+        nc.vector.tensor_tensor(mean_gain[:], mean[:], gain[:], ALU.mult)
+        shift = held.tile([P, Q_BLOCKS], F32, name="shift")
+        nc.vector.tensor_tensor(shift[:], beta_t[:], mean_gain[:], ALU.subtract)
+
+        with tc.psum_pool(name="turned_banks", bufs=8 - GRAM_BANKS) as turned_banks:
+            for b in range(GRAPHS):
+                for j in range(Q_BLOCKS):
+                    r_turned = turned_banks.tile([P, NODES], BF16, name="r_turned")
+                    for n in range(NODE_BLOCKS):
+                        nc.tensor.transpose(
+                            r_turned[:, n * P : (n + 1) * P], r_tiles[b][n][:, j, 0:P], ident_bf[:]
+                        )
+                    y = results.tile([P, NODES], F32, name="y")
+                    if j % 2 == 0:
+                        nc.scalar.activation(
+                            y[:],
+                            r_turned[:],
+                            FUNC.Identity,
+                            bias=shift[:, j : j + 1],
+                            scale=gain[:, j : j + 1],
+                        )
+                    else:
+                        nc.vector.tensor_scalar(
+                            y[:],
+                            r_turned[:],
+                            gain[:, j : j + 1],
+                            shift[:, j : j + 1],
+                            ALU.mult,
+                            ALU.add,
+                        )
+                    row = (b * Q_BLOCKS + j) * P
+                    nc.sync.dma_start(out[row : row + P, :], y[:])

@@ -21,6 +21,7 @@ HALF_BLOCKS = F_OUT // P
 WIDE = 512
 NARROW = 256
 GROUP = 2
+H_BUFS = {"self": 3, "nei": 2}
 COUNT = GRAPHS * NODES
 EPS = 1e-5
 
@@ -37,18 +38,19 @@ def tile_batchedgraphsagemean1_b_kernel(
     nc = tc.nc
     with (
         tc.tile_pool(name="held", bufs=1) as held,
-        tc.tile_pool(name="sums", bufs=3 * F_BLOCKS) as sums,
-        tc.tile_pool(name="means", bufs=2 * F_BLOCKS) as means,
+        tc.tile_pool(name="sums", bufs=5 * F_BLOCKS) as sums,
+        tc.tile_pool(name="means", bufs=F_BLOCKS) as means,
         tc.tile_pool(name="small", bufs=3 * GROUP) as small,
         tc.tile_pool(name="scratch", bufs=2) as scratch,
-        tc.tile_pool(name="results", bufs=6) as results,
+        tc.tile_pool(name="results", bufs=8) as results,
         tc.psum_pool(name="gram_banks", bufs=1) as gram_banks,
     ):
         lists = held.tile([P, NEIGHBOURS * NODES // 16], U16, name="lists")
         nc.sync.dma_start(lists[:], offs)
         x_f32 = [held.tile([P, NODES], F32, name=f"x_f32_{i}") for i in range(GRAPHS * F_BLOCKS)]
+        load_queues = (nc.scalar, nc.sync)
         for i in range(F_BLOCKS):
-            nc.sync.dma_start(x_f32[i][:], x[i * P : (i + 1) * P, :])
+            load_queues[i % 2].dma_start(x_f32[i][:], x[i * P : (i + 1) * P, :])
         weights = {}
         for part, w in (("self", w_self), ("nei", w_nei)):
             weights[part] = held.tile([P, F_BLOCKS, F_OUT], BF16, name=f"w_{part}")
@@ -59,10 +61,10 @@ def tile_batchedgraphsagemean1_b_kernel(
         bias_f32 = held.tile([1, CHANNELS], F32, name="bias_f32")
         nc.scalar.dma_start(bias_f32[:, 0:F_OUT], bias_self.rearrange("q o -> o q"))
         nc.scalar.dma_start(bias_f32[:, F_OUT:CHANNELS], bias_nei.rearrange("q o -> o q"))
-        gamma_t = held.tile([P, Q_BLOCKS], F32, name="gamma_t")
+        gamma_pair = held.tile([P, 2, Q_BLOCKS], F32, name="gamma_pair")
         beta_t = held.tile([P, Q_BLOCKS], F32, name="beta_t")
         with nc.allow_non_contiguous_dma(reason="one 4-byte value to a partition, 8 KiB in all"):
-            nc.scalar.dma_start(gamma_t[:], gamma.rearrange("(j p) o -> p (j o)", p=P))
+            nc.scalar.dma_start(gamma_pair[:, 0, :], gamma.rearrange("(j p) o -> p (j o)", p=P))
             nc.scalar.dma_start(beta_t[:], beta.rearrange("(j p) o -> p (j o)", p=P))
 
         zeros = held.tile([P, WIDE], F32, name="zeros")
@@ -85,7 +87,7 @@ def tile_batchedgraphsagemean1_b_kernel(
         ]
         for b in range(GRAPHS):
             for n in range(NODE_BLOCKS):
-                nc.gpsimd.memset(r_tiles[b][n][:, :, P : P + 1], 1.0)
+                nc.vector.memset(r_tiles[b][n][:, :, P : P + 1], 1.0)
 
         x_bf = [held.tile([P, NODES], BF16, name=f"x_bf_{i}") for i in range(GRAPHS * F_BLOCKS)]
         for i in range(GRAPHS * F_BLOCKS):
@@ -103,7 +105,7 @@ def tile_batchedgraphsagemean1_b_kernel(
         with tc.psum_pool(name="h_banks", bufs=GROUP) as h_banks:
 
             def project(part, half, nodes_of):
-                h_half = h_banks.tile([P, F_OUT], F32, name=f"h_{part}")
+                h_half = h_banks.tile([P, F_OUT], F32, name=f"h_{part}", bufs=H_BUFS[part])
                 nc.tensor.matmul(
                     h_half[:],
                     lhsT=first_row[:],
@@ -125,20 +127,69 @@ def tile_batchedgraphsagemean1_b_kernel(
                 squares = scratch.tile([P, F_OUT], BF16, name="squares")
                 nc.scalar.activation(squares[:], h_half[:], FUNC.Square, accum_out=total)
 
-            def begin(block):
-                b, n = block
-                h_self = project(
-                    "self", 0, [x_bf[b * F_BLOCKS + f][:, n * P : (n + 1) * P] for f in range(F_BLOCKS)]
+            h_self, h_nei, square_sums = {}, {}, {}
+
+            def project_self(i):
+                b, n = blocks[i]
+                in_x = slice(n * P, (n + 1) * P)
+                h_self[i] = project("self", 0, [x_bf[b * F_BLOCKS + f][:, in_x] for f in range(F_BLOCKS)])
+                square_sums[i] = small.tile([P, 2], F32, name="square_sums")
+
+            def normalise(i):
+                inv_norm = small.tile([P, 1], F32, name="inv_norm")
+                nc.scalar.activation(
+                    inv_norm[:],
+                    square_sums[i][:, 0:1],
+                    FUNC.Abs_reciprocal_sqrt,
+                    bias=square_sums[i][:, 1:2],
                 )
-                square_sums = small.tile([P, 2], F32, name="square_sums")
-                sum_of_squares(h_self, square_sums[:, 0:1])
-                return h_self, square_sums
+                b, n = blocks[i]
+                r = r_tiles[b][n]
+                nc.scalar.activation(
+                    r[:, 0:HALF_BLOCKS, 0:P],
+                    h_self[i][:].rearrange("p (j c) -> p j c", c=P),
+                    FUNC.Relu,
+                    scale=inv_norm[:, 0:1],
+                )
+                if i < len(blocks) - NARROW // P:
+                    nc.scalar.activation(
+                        r[:, HALF_BLOCKS:Q_BLOCKS, 0:P],
+                        h_nei[i][:].rearrange("p (j c) -> p j c", c=P),
+                        FUNC.Relu,
+                        scale=inv_norm[:, 0:1],
+                    )
+                else:
+                    nc.vector.tensor_scalar(
+                        r[:, HALF_BLOCKS:Q_BLOCKS, 0:P],
+                        h_nei[i][:].rearrange("p (j c) -> p j c", c=P),
+                        inv_norm[:, 0:1],
+                        0.0,
+                        ALU.mult,
+                        ALU.max,
+                    )
 
-            begun = {}
-            for block in blocks[0:GROUP]:
-                begun[block] = begin(block)
+            def add_to_batch_sums(i):
+                b, n = blocks[i]
+                r = r_tiles[b][n]
+                for j in range(Q_BLOCKS):
+                    place = (j % GRAMS_IN_BANK) * R_STEP
+                    last_in_bank = j % GRAMS_IN_BANK == GRAMS_IN_BANK - 1 or j == Q_BLOCKS - 1
+                    nc.tensor.matmul(
+                        grams[j // GRAMS_IN_BANK][:, place : place + P + 1],
+                        lhsT=r[:, j, 0:P],
+                        rhs=r[:, j, 0 : P + 1],
+                        start=(i == 0 and j % GRAMS_IN_BANK == 0),
+                        stop=(i == len(blocks) - 1 and last_in_bank),
+                    )
 
+            for i in range(GROUP):
+                project_self(i)
+            for i in range(GROUP):
+                sum_of_squares(h_self[i], square_sums[i][:, 0:1])
+
+            i1 = 0
             for b, c0, width in pieces:
+                i0, i1 = i1, i1 + width // P
                 running = [zeros[:, 0:width] for f in range(F_BLOCKS)]
                 for k in range(NEIGHBOURS):
                     first = (k * NODES + c0) // 16
@@ -151,110 +202,114 @@ def tile_batchedgraphsagemean1_b_kernel(
                         running[f] = longer[:]
                 agg_bf = [means.tile([P, width], BF16, name="agg_bf") for f in range(F_BLOCKS)]
                 for f in range(F_BLOCKS):
-                    nc.scalar.activation(agg_bf[f][:], running[f], FUNC.Copy, scale=1.0 / NEIGHBOURS)
-
-                for n0 in range(c0 // P, (c0 + width) // P, GROUP):
-                    group = [(b, n) for n in range(n0, n0 + GROUP)]
-                    h_nei = {}
-                    for block in group:
-                        in_piece = slice(block[1] * P - c0, (block[1] + 1) * P - c0)
-                        h_nei[block] = project(
-                            "nei", 1, [agg_bf[f][:, in_piece] for f in range(F_BLOCKS)]
-                        )
-                    for block in group:
-                        h_self, square_sums = begun[block]
-                        sum_of_squares(h_nei[block], square_sums[:, 1:2])
-                        inv_norm = small.tile([P, 1], F32, name="inv_norm")
+                    if i1 < len(blocks):
                         nc.scalar.activation(
-                            inv_norm[:],
-                            square_sums[:, 0:1],
-                            FUNC.Abs_reciprocal_sqrt,
-                            bias=square_sums[:, 1:2],
-                        )
-                        r = r_tiles[block[0]][block[1]]
-                        for half, h_half in enumerate((h_self, h_nei[block])):
-                            nc.scalar.activation(
-                                r[:, half * HALF_BLOCKS : (half + 1) * HALF_BLOCKS, 0:P],
-                                h_half[:].rearrange("p (j c) -> p j c", c=P),
-                                FUNC.Relu,
-                                scale=inv_norm[:, 0:1],
-                            )
-                    for block in group:
-                        r = r_tiles[block[0]][block[1]]
-                        turn = blocks.index(block)
-                        for j in range(Q_BLOCKS):
-                            place = (j % GRAMS_IN_BANK) * R_STEP
-                            last_in_bank = j % GRAMS_IN_BANK == GRAMS_IN_BANK - 1 or j == Q_BLOCKS - 1
-                            nc.tensor.matmul(
-                                grams[j // GRAMS_IN_BANK][:, place : place + P + 1],
-                                lhsT=r[:, j, 0:P],
-                                rhs=r[:, j, 0 : P + 1],
-                                start=(turn == 0 and j % GRAMS_IN_BANK == 0),
-                                stop=(turn == len(blocks) - 1 and last_in_bank),
-                            )
-                        if turn + GROUP < len(blocks):
-                            begun[blocks[turn + GROUP]] = begin(blocks[turn + GROUP])
-
-        mean = held.tile([P, Q_BLOCKS], F32, name="mean")
-        mean_of_squares = held.tile([P, Q_BLOCKS], F32, name="mean_of_squares")
-        for t in range(GRAM_BANKS):
-            in_bank = min(GRAMS_IN_BANK, Q_BLOCKS - t * GRAMS_IN_BANK)
-            nc.scalar.activation(
-                mean[:, t * GRAMS_IN_BANK : t * GRAMS_IN_BANK + in_bank],
-                grams[t][:, P : P + (in_bank - 1) * R_STEP + 1 : R_STEP],
-                FUNC.Copy,
-                scale=1.0 / COUNT,
-            )
-        square_of_mean = held.tile([P, Q_BLOCKS], F32, name="square_of_mean")
-        nc.scalar.activation(square_of_mean[:], mean[:], FUNC.Square)
-        for j in range(Q_BLOCKS):
-            place = (j % GRAMS_IN_BANK) * R_STEP
-            diagonal = scratch.tile([P, P], F32, name="diagonal")
-            nc.vector.scalar_tensor_tensor(
-                out=diagonal[:],
-                in0=grams[j // GRAMS_IN_BANK][:, place : place + P],
-                scalar=1.0 / COUNT,
-                in1=ident_f32[:],
-                op0=ALU.mult,
-                op1=ALU.mult,
-                accum_out=mean_of_squares[:, j : j + 1],
-            )
-        variance = held.tile([P, Q_BLOCKS], F32, name="variance")
-        nc.vector.tensor_tensor(variance[:], mean_of_squares[:], square_of_mean[:], ALU.subtract)
-        inv_std = held.tile([P, Q_BLOCKS], F32, name="inv_std")
-        nc.scalar.activation(inv_std[:], variance[:], FUNC.Abs_reciprocal_sqrt, bias=eps_t[:, 0:1])
-        gain = held.tile([P, Q_BLOCKS], F32, name="gain")
-        nc.vector.tensor_tensor(gain[:], gamma_t[:], inv_std[:], ALU.mult)
-        mean_gain = held.tile([P, Q_BLOCKS], F32, name="mean_gain")
-        nc.vector.tensor_tensor(mean_gain[:], mean[:], gain[:], ALU.mult)
-        shift = held.tile([P, Q_BLOCKS], F32, name="shift")
-        nc.vector.tensor_tensor(shift[:], beta_t[:], mean_gain[:], ALU.subtract)
-
-        with tc.psum_pool(name="turned_banks", bufs=8 - GRAM_BANKS) as turned_banks:
-            for b in range(GRAPHS):
-                for j in range(Q_BLOCKS):
-                    r_turned = turned_banks.tile([P, NODES], BF16, name="r_turned")
-                    for n in range(NODE_BLOCKS):
-                        nc.tensor.transpose(
-                            r_turned[:, n * P : (n + 1) * P], r_tiles[b][n][:, j, 0:P], ident_bf[:]
-                        )
-                    y = results.tile([P, NODES], F32, name="y")
-                    if j % 2 == 0:
-                        nc.scalar.activation(
-                            y[:],
-                            r_turned[:],
-                            FUNC.Identity,
-                            bias=shift[:, j : j + 1],
-                            scale=gain[:, j : j + 1],
+                            agg_bf[f][:], running[f], FUNC.Copy, scale=1.0 / NEIGHBOURS
                         )
                     else:
                         nc.vector.tensor_scalar(
-                            y[:],
-                            r_turned[:],
-                            gain[:, j : j + 1],
-                            shift[:, j : j + 1],
-                            ALU.mult,
-                            ALU.add,
+                            agg_bf[f][:], running[f], 1.0 / NEIGHBOURS, None, ALU.mult
                         )
-                    row = (b * Q_BLOCKS + j) * P
-                    nc.sync.dma_start(out[row : row + P, :], y[:])
+
+                def project_nei(i):
+                    in_piece = slice((i - i0) * P, (i - i0 + 1) * P)
+                    h_nei[i] = project("nei", 1, [agg_bf[f][:, in_piece] for f in range(F_BLOCKS)])
+
+                for i in range(i0, i0 + GROUP):
+                    project_nei(i)
+                for i in range(max(i0 - GROUP, 0), i0):
+                    add_to_batch_sums(i)
+                for i in range(i0, i1):
+                    if i >= i0 + GROUP:
+                        sum_of_squares(h_self[i], square_sums[i][:, 0:1])
+                    sum_of_squares(h_nei[i], square_sums[i][:, 1:2])
+                    normalise(i)
+                    if i + GROUP < len(blocks):
+                        project_self(i + GROUP)
+                    if i + GROUP < i1:
+                        project_nei(i + GROUP)
+                        add_to_batch_sums(i)
+                for i in range(i1, min(i1 + GROUP, len(blocks))):
+                    sum_of_squares(h_self[i], square_sums[i][:, 0:1])
+            for i in range(len(blocks) - GROUP, len(blocks)):
+                add_to_batch_sums(i)
+
+        mean = held.tile([P, Q_BLOCKS], F32, name="mean")
+        square_of_mean = held.tile([P, Q_BLOCKS], F32, name="square_of_mean")
+        mean_of_squares = held.tile([P, Q_BLOCKS], F32, name="mean_of_squares")
+        variance = held.tile([P, Q_BLOCKS], F32, name="variance")
+        inv_std = held.tile([P, 1, Q_BLOCKS], F32, name="inv_std")
+        gain_pair = held.tile([P, 2, Q_BLOCKS], F32, name="gain_pair")
+        shift = held.tile([P, Q_BLOCKS], F32, name="shift")
+        with tc.psum_pool(name="turned_banks", bufs=8 - GRAM_BANKS) as turned_banks:
+            for t in range(GRAM_BANKS):
+                in_bank = min(GRAMS_IN_BANK, Q_BLOCKS - t * GRAMS_IN_BANK)
+                these = slice(t * GRAMS_IN_BANK, t * GRAMS_IN_BANK + in_bank)
+                nc.scalar.activation(
+                    mean[:, these],
+                    grams[t][:, P : P + (in_bank - 1) * R_STEP + 1 : R_STEP],
+                    FUNC.Copy,
+                    scale=1.0 / COUNT,
+                )
+                nc.scalar.activation(square_of_mean[:, these], mean[:, these], FUNC.Square)
+                for j in range(these.start, these.stop):
+                    place = (j % GRAMS_IN_BANK) * R_STEP
+                    diagonal = scratch.tile([P, P], F32, name="diagonal")
+                    nc.vector.scalar_tensor_tensor(
+                        out=diagonal[:],
+                        in0=grams[t][:, place : place + P],
+                        scalar=1.0 / COUNT,
+                        in1=ident_f32[:],
+                        op0=ALU.mult,
+                        op1=ALU.mult,
+                        accum_out=mean_of_squares[:, j : j + 1],
+                    )
+                nc.vector.tensor_tensor(
+                    variance[:, these], mean_of_squares[:, these], square_of_mean[:, these], ALU.subtract
+                )
+                nc.scalar.activation(
+                    inv_std[:, 0, these],
+                    variance[:, these],
+                    FUNC.Abs_reciprocal_sqrt,
+                    bias=eps_t[:, 0:1],
+                )
+                nc.vector.tensor_tensor(
+                    gamma_pair[:, 1, these], mean[:, these], gamma_pair[:, 0, these], ALU.mult
+                )
+                nc.vector.tensor_tensor(
+                    gain_pair[:, :, these],
+                    gamma_pair[:, :, these],
+                    inv_std[:, :, these].to_broadcast([P, 2, in_bank]),
+                    ALU.mult,
+                )
+                nc.vector.tensor_tensor(
+                    shift[:, these], beta_t[:, these], gain_pair[:, 1, these], ALU.subtract
+                )
+
+                for j in range(these.start, these.stop):
+                    for b in range(GRAPHS):
+                        r_turned = turned_banks.tile([P, NODES], BF16, name="r_turned")
+                        for n in range(NODE_BLOCKS):
+                            nc.tensor.transpose(
+                                r_turned[:, n * P : (n + 1) * P], r_tiles[b][n][:, j, 0:P], ident_bf[:]
+                            )
+                        y = results.tile([P, NODES], F32, name="y")
+                        if b == 0:
+                            nc.scalar.activation(
+                                y[:],
+                                r_turned[:],
+                                FUNC.Identity,
+                                bias=shift[:, j : j + 1],
+                                scale=gain_pair[:, 0, j : j + 1],
+                            )
+                        else:
+                            nc.vector.tensor_scalar(
+                                y[:],
+                                r_turned[:],
+                                gain_pair[:, 0, j : j + 1],
+                                shift[:, j : j + 1],
+                                ALU.mult,
+                                ALU.add,
+                            )
+                        row = (b * Q_BLOCKS + j) * P
+                        nc.sync.dma_start(out[row : row + P, :], y[:])

@@ -42,7 +42,7 @@ def tile_batchedgraphsagemean1_b_kernel(
         tc.tile_pool(name="means", bufs=F_BLOCKS) as means,
         tc.tile_pool(name="small", bufs=3 * GROUP) as small,
         tc.tile_pool(name="scratch", bufs=2) as scratch,
-        tc.tile_pool(name="results", bufs=8) as results,
+        tc.tile_pool(name="results", bufs=4) as results,
         tc.psum_pool(name="gram_banks", bufs=1) as gram_banks,
     ):
         lists = held.tile([P, NEIGHBOURS * NODES // 16], U16, name="lists")
@@ -61,16 +61,14 @@ def tile_batchedgraphsagemean1_b_kernel(
         bias_f32 = held.tile([1, CHANNELS], F32, name="bias_f32")
         nc.scalar.dma_start(bias_f32[:, 0:F_OUT], bias_self.rearrange("q o -> o q"))
         nc.scalar.dma_start(bias_f32[:, F_OUT:CHANNELS], bias_nei.rearrange("q o -> o q"))
-        gamma_pair = held.tile([P, 2, Q_BLOCKS], F32, name="gamma_pair")
+        gamma_t = held.tile([P, Q_BLOCKS], F32, name="gamma_t")
         beta_t = held.tile([P, Q_BLOCKS], F32, name="beta_t")
         with nc.allow_non_contiguous_dma(reason="one 4-byte value to a partition, 8 KiB in all"):
-            nc.scalar.dma_start(gamma_pair[:, 0, :], gamma.rearrange("(j p) o -> p (j o)", p=P))
+            nc.scalar.dma_start(gamma_t[:], gamma.rearrange("(j p) o -> p (j o)", p=P))
             nc.scalar.dma_start(beta_t[:], beta.rearrange("(j p) o -> p (j o)", p=P))
 
         zeros = held.tile([P, WIDE], F32, name="zeros")
         nc.gpsimd.memset(zeros[:], 0.0)
-        eps_t = held.tile([P, 1], F32, name="eps_t")
-        nc.gpsimd.memset(eps_t[:], EPS)
         ident_bf = held.tile([P, P], BF16, name="ident_bf")
         make_identity(nc, ident_bf[:])
         ident_f32 = held.tile([P, P], F32, name="ident_f32")
@@ -236,23 +234,22 @@ def tile_batchedgraphsagemean1_b_kernel(
 
         mean = held.tile([P, Q_BLOCKS], F32, name="mean")
         square_of_mean = held.tile([P, Q_BLOCKS], F32, name="square_of_mean")
+        eps_less_square = held.tile([P, Q_BLOCKS], F32, name="eps_less_square")
+        minus_mean_gamma = held.tile([P, Q_BLOCKS], F32, name="minus_mean_gamma")
         mean_of_squares = held.tile([P, Q_BLOCKS], F32, name="mean_of_squares")
-        variance = held.tile([P, Q_BLOCKS], F32, name="variance")
-        inv_std = held.tile([P, 1, Q_BLOCKS], F32, name="inv_std")
-        gain_pair = held.tile([P, 2, Q_BLOCKS], F32, name="gain_pair")
+        inv_std = held.tile([P, Q_BLOCKS], F32, name="inv_std")
+        gain = held.tile([P, Q_BLOCKS], F32, name="gain")
         shift = held.tile([P, Q_BLOCKS], F32, name="shift")
+        out_blocks = out.rearrange("(b j p) s -> j p b s", b=GRAPHS, p=P)
         with tc.psum_pool(name="turned_banks", bufs=8 - GRAM_BANKS) as turned_banks:
             for t in range(GRAM_BANKS):
                 in_bank = min(GRAMS_IN_BANK, Q_BLOCKS - t * GRAMS_IN_BANK)
                 these = slice(t * GRAMS_IN_BANK, t * GRAMS_IN_BANK + in_bank)
-                nc.scalar.activation(
-                    mean[:, these],
-                    grams[t][:, P : P + (in_bank - 1) * R_STEP + 1 : R_STEP],
-                    FUNC.Copy,
-                    scale=1.0 / COUNT,
-                )
-                nc.scalar.activation(square_of_mean[:, these], mean[:, these], FUNC.Square)
+                sums_of_r = grams[t][:, P : P + (in_bank - 1) * R_STEP + 1 : R_STEP]
+                nc.scalar.activation(square_of_mean[:, these], sums_of_r, FUNC.Square, scale=1.0 / COUNT)
+                nc.scalar.activation(mean[:, these], sums_of_r, FUNC.Copy, scale=1.0 / COUNT)
                 for j in range(these.start, these.stop):
+                    column = slice(j, j + 1)
                     place = (j % GRAMS_IN_BANK) * R_STEP
                     diagonal = scratch.tile([P, P], F32, name="diagonal")
                     nc.vector.scalar_tensor_tensor(
@@ -262,54 +259,54 @@ def tile_batchedgraphsagemean1_b_kernel(
                         in1=ident_f32[:],
                         op0=ALU.mult,
                         op1=ALU.mult,
-                        accum_out=mean_of_squares[:, j : j + 1],
+                        accum_out=mean_of_squares[:, column],
                     )
-                nc.vector.tensor_tensor(
-                    variance[:, these], mean_of_squares[:, these], square_of_mean[:, these], ALU.subtract
-                )
-                nc.scalar.activation(
-                    inv_std[:, 0, these],
-                    variance[:, these],
-                    FUNC.Abs_reciprocal_sqrt,
-                    bias=eps_t[:, 0:1],
-                )
-                nc.vector.tensor_tensor(
-                    gamma_pair[:, 1, these], mean[:, these], gamma_pair[:, 0, these], ALU.mult
-                )
-                nc.vector.tensor_tensor(
-                    gain_pair[:, :, these],
-                    gamma_pair[:, :, these],
-                    inv_std[:, :, these].to_broadcast([P, 2, in_bank]),
-                    ALU.mult,
-                )
-                nc.vector.tensor_tensor(
-                    shift[:, these], beta_t[:, these], gain_pair[:, 1, these], ALU.subtract
-                )
+                    if j == these.start:
+                        nc.vector.tensor_scalar(
+                            eps_less_square[:, these], square_of_mean[:, these], -1.0, EPS, ALU.mult, ALU.add
+                        )
+                        nc.vector.scalar_tensor_tensor(
+                            out=minus_mean_gamma[:, these],
+                            in0=mean[:, these],
+                            scalar=-1.0,
+                            in1=gamma_t[:, these],
+                            op0=ALU.mult,
+                            op1=ALU.mult,
+                        )
+                    nc.scalar.activation(
+                        inv_std[:, column],
+                        mean_of_squares[:, column],
+                        FUNC.Abs_reciprocal_sqrt,
+                        bias=eps_less_square[:, column],
+                    )
+                    nc.scalar.activation(
+                        gain[:, column], gamma_t[:, column], FUNC.Copy, scale=inv_std[:, column]
+                    )
+                    nc.scalar.activation(
+                        shift[:, column],
+                        minus_mean_gamma[:, column],
+                        FUNC.Identity,
+                        bias=beta_t[:, column],
+                        scale=inv_std[:, column],
+                    )
 
-                for j in range(these.start, these.stop):
+                    y = results.tile([P, GRAPHS, NODES], F32, name="y")
                     for b in range(GRAPHS):
                         r_turned = turned_banks.tile([P, NODES], BF16, name="r_turned")
                         for n in range(NODE_BLOCKS):
                             nc.tensor.transpose(
                                 r_turned[:, n * P : (n + 1) * P], r_tiles[b][n][:, j, 0:P], ident_bf[:]
                             )
-                        y = results.tile([P, NODES], F32, name="y")
                         if b == 0:
                             nc.scalar.activation(
-                                y[:],
+                                y[:, b, :],
                                 r_turned[:],
                                 FUNC.Identity,
-                                bias=shift[:, j : j + 1],
-                                scale=gain_pair[:, 0, j : j + 1],
+                                bias=shift[:, column],
+                                scale=gain[:, column],
                             )
                         else:
                             nc.vector.tensor_scalar(
-                                y[:],
-                                r_turned[:],
-                                gain_pair[:, 0, j : j + 1],
-                                shift[:, j : j + 1],
-                                ALU.mult,
-                                ALU.add,
+                                y[:, b, :], r_turned[:], gain[:, column], shift[:, column], ALU.mult, ALU.add
                             )
-                        row = (b * Q_BLOCKS + j) * P
-                        nc.sync.dma_start(out[row : row + P, :], y[:])
+                    nc.sync.dma_start(out_blocks[j], y[:])

@@ -18,8 +18,8 @@ F_BLOCKS = F_IN // P
 Q_BLOCKS = CHANNELS // P
 NODE_BLOCKS = NODES // P
 HALF_BLOCKS = F_OUT // P
-WIDE = 512
-NARROW = 256
+PIECE_WIDTHS = ((512, 512), (384, 256, 256, 128))
+WIDEST = 512
 GROUP = 2
 H_BUFS = {"self": 3, "nei": 2}
 COUNT = GRAPHS * NODES
@@ -67,7 +67,7 @@ def tile_batchedgraphsagemean1_b_kernel(
             nc.scalar.dma_start(gamma_t[:], gamma.rearrange("(j p) o -> p (j o)", p=P))
             nc.scalar.dma_start(beta_t[:], beta.rearrange("(j p) o -> p (j o)", p=P))
 
-        zeros = held.tile([P, WIDE], F32, name="zeros")
+        zeros = held.tile([P, WIDEST], F32, name="zeros")
         nc.gpsimd.memset(zeros[:], 0.0)
         ident_bf = held.tile([P, P], BF16, name="ident_bf")
         make_identity(nc, ident_bf[:])
@@ -96,8 +96,12 @@ def tile_batchedgraphsagemean1_b_kernel(
             for t in range(GRAM_BANKS)
         ]
 
-        pieces = [(0, c0, WIDE) for c0 in range(0, NODES, WIDE)]
-        pieces += [(1, c0, NARROW) for c0 in range(0, NODES, NARROW)]
+        pieces = [
+            (b, sum(PIECE_WIDTHS[b][:t]), width)
+            for b in range(GRAPHS)
+            for t, width in enumerate(PIECE_WIDTHS[b])
+        ]
+        last_piece_blocks = pieces[-1][2] // P
         blocks = [(b, n) for b, c0, width in pieces for n in range(c0 // P, (c0 + width) // P)]
 
         with tc.psum_pool(name="h_banks", bufs=GROUP) as h_banks:
@@ -126,12 +130,19 @@ def tile_batchedgraphsagemean1_b_kernel(
                 nc.scalar.activation(squares[:], h_half[:], FUNC.Square, accum_out=total)
 
             h_self, h_nei, square_sums = {}, {}, {}
+            self_squared = []
+            not_yet_added = []
 
             def project_self(i):
                 b, n = blocks[i]
                 in_x = slice(n * P, (n + 1) * P)
                 h_self[i] = project("self", 0, [x_bf[b * F_BLOCKS + f][:, in_x] for f in range(F_BLOCKS)])
                 square_sums[i] = small.tile([P, 2], F32, name="square_sums")
+
+            def square_self_up_to(last):
+                for i in range(len(self_squared), last + 1):
+                    sum_of_squares(h_self[i], square_sums[i][:, 0:1])
+                    self_squared.append(i)
 
             def normalise(i):
                 inv_norm = small.tile([P, 1], F32, name="inv_norm")
@@ -149,7 +160,7 @@ def tile_batchedgraphsagemean1_b_kernel(
                     FUNC.Relu,
                     scale=inv_norm[:, 0:1],
                 )
-                if i < len(blocks) - NARROW // P:
+                if i < len(blocks) - last_piece_blocks:
                     nc.scalar.activation(
                         r[:, HALF_BLOCKS:Q_BLOCKS, 0:P],
                         h_nei[i][:].rearrange("p (j c) -> p j c", c=P),
@@ -182,8 +193,7 @@ def tile_batchedgraphsagemean1_b_kernel(
 
             for i in range(GROUP):
                 project_self(i)
-            for i in range(GROUP):
-                sum_of_squares(h_self[i], square_sums[i][:, 0:1])
+            square_self_up_to(GROUP - 1)
 
             i1 = 0
             for b, c0, width in pieces:
@@ -213,13 +223,13 @@ def tile_batchedgraphsagemean1_b_kernel(
                     in_piece = slice((i - i0) * P, (i - i0 + 1) * P)
                     h_nei[i] = project("nei", 1, [agg_bf[f][:, in_piece] for f in range(F_BLOCKS)])
 
-                for i in range(i0, i0 + GROUP):
+                for i in range(i0, min(i0 + GROUP, i1)):
                     project_nei(i)
-                for i in range(max(i0 - GROUP, 0), i0):
+                for i in not_yet_added:
                     add_to_batch_sums(i)
+                not_yet_added.clear()
                 for i in range(i0, i1):
-                    if i >= i0 + GROUP:
-                        sum_of_squares(h_self[i], square_sums[i][:, 0:1])
+                    square_self_up_to(i)
                     sum_of_squares(h_nei[i], square_sums[i][:, 1:2])
                     normalise(i)
                     if i + GROUP < len(blocks):
@@ -227,9 +237,10 @@ def tile_batchedgraphsagemean1_b_kernel(
                     if i + GROUP < i1:
                         project_nei(i + GROUP)
                         add_to_batch_sums(i)
-                for i in range(i1, min(i1 + GROUP, len(blocks))):
-                    sum_of_squares(h_self[i], square_sums[i][:, 0:1])
-            for i in range(len(blocks) - GROUP, len(blocks)):
+                    else:
+                        not_yet_added.append(i)
+                square_self_up_to(min(i1 + GROUP, len(blocks)) - 1)
+            for i in not_yet_added:
                 add_to_batch_sums(i)
 
         mean = held.tile([P, Q_BLOCKS], F32, name="mean")

@@ -20,14 +20,16 @@ NODE_BLOCKS = NODES // P
 HALF_BLOCKS = F_OUT // P
 PIECE_WIDTHS = ((512, 512), (384, 256, 256, 128))
 WIDEST = 512
+ROUNDED_BY_VECTOR = 2
 GROUP = 2
-H_BUFS = {"self": 3, "nei": 2}
+H_BUFS = {"self": 2, "nei": 3}
 COUNT = GRAPHS * NODES
 EPS = 1e-5
 
 R_STEP = P + 2
 GRAMS_IN_BANK = 3
-GRAM_BANKS = 3
+BLOCKS_OF_GRAM_BANK = ((0, 1), (2, 3, 4), (5, 6, 7))
+GRAM_BANKS = len(BLOCKS_OF_GRAM_BANK)
 
 FLOPS = 2 * GRAPHS * NODES * F_IN * CHANNELS
 
@@ -95,6 +97,12 @@ def tile_batchedgraphsagemean1_b_kernel(
             gram_banks.tile([P, GRAMS_IN_BANK * R_STEP], F32, name=f"gram_{t}")
             for t in range(GRAM_BANKS)
         ]
+        gram_bank_of = {j: t for t in range(GRAM_BANKS) for j in BLOCKS_OF_GRAM_BANK[t]}
+        gram_of = {
+            j: grams[t][:, a * R_STEP : a * R_STEP + P + 1]
+            for t in range(GRAM_BANKS)
+            for a, j in enumerate(BLOCKS_OF_GRAM_BANK[t])
+        }
 
         pieces = [
             (b, sum(PIECE_WIDTHS[b][:t]), width)
@@ -102,6 +110,7 @@ def tile_batchedgraphsagemean1_b_kernel(
             for t, width in enumerate(PIECE_WIDTHS[b])
         ]
         last_piece_blocks = pieces[-1][2] // P
+        first_rounded_by_vector = len(pieces) - ROUNDED_BY_VECTOR
         blocks = [(b, n) for b, c0, width in pieces for n in range(c0 // P, (c0 + width) // P)]
 
         with tc.psum_pool(name="h_banks", bufs=GROUP) as h_banks:
@@ -154,12 +163,15 @@ def tile_batchedgraphsagemean1_b_kernel(
                 )
                 b, n = blocks[i]
                 r = r_tiles[b][n]
-                nc.scalar.activation(
-                    r[:, 0:HALF_BLOCKS, 0:P],
-                    h_self[i][:].rearrange("p (j c) -> p j c", c=P),
-                    FUNC.Relu,
-                    scale=inv_norm[:, 0:1],
-                )
+                first_bank = len(BLOCKS_OF_GRAM_BANK[0])
+                steps = ((0, HALF_BLOCKS),) if i < len(blocks) - 1 else ((0, first_bank), (first_bank, HALF_BLOCKS))
+                for j0, j1 in steps:
+                    nc.scalar.activation(
+                        r[:, j0:j1, 0:P],
+                        h_self[i][:, j0 * P : j1 * P].rearrange("p (j c) -> p j c", c=P),
+                        FUNC.Relu,
+                        scale=inv_norm[:, 0:1],
+                    )
                 if i < len(blocks) - last_piece_blocks:
                     nc.scalar.activation(
                         r[:, HALF_BLOCKS:Q_BLOCKS, 0:P],
@@ -181,14 +193,13 @@ def tile_batchedgraphsagemean1_b_kernel(
                 b, n = blocks[i]
                 r = r_tiles[b][n]
                 for j in range(Q_BLOCKS):
-                    place = (j % GRAMS_IN_BANK) * R_STEP
-                    last_in_bank = j % GRAMS_IN_BANK == GRAMS_IN_BANK - 1 or j == Q_BLOCKS - 1
+                    in_bank = BLOCKS_OF_GRAM_BANK[gram_bank_of[j]]
                     nc.tensor.matmul(
-                        grams[j // GRAMS_IN_BANK][:, place : place + P + 1],
+                        gram_of[j],
                         lhsT=r[:, j, 0:P],
                         rhs=r[:, j, 0 : P + 1],
-                        start=(i == 0 and j % GRAMS_IN_BANK == 0),
-                        stop=(i == len(blocks) - 1 and last_in_bank),
+                        start=(i == 0 and j == in_bank[0]),
+                        stop=(i == len(blocks) - 1 and j == in_bank[-1]),
                     )
 
             for i in range(GROUP):
@@ -196,9 +207,20 @@ def tile_batchedgraphsagemean1_b_kernel(
             square_self_up_to(GROUP - 1)
 
             i1 = 0
-            for b, c0, width in pieces:
+            for t, (b, c0, width) in enumerate(pieces):
                 i0, i1 = i1, i1 + width // P
+                by_vector = t >= first_rounded_by_vector
+                if by_vector:
+                    agg_bf = [
+                        held.tile([P, width], BF16, name=f"agg_bf_{t}_{f}") for f in range(F_BLOCKS)
+                    ]
+                else:
+                    agg_bf = [means.tile([P, width], BF16, name="agg_bf") for f in range(F_BLOCKS)]
                 running = [zeros[:, 0:width] for f in range(F_BLOCKS)]
+
+                def round_on_vector(f):
+                    nc.vector.tensor_scalar(agg_bf[f][:], running[f], 1.0 / NEIGHBOURS, None, ALU.mult)
+
                 for k in range(NEIGHBOURS):
                     first = (k * NODES + c0) // 16
                     piece = lists[:, first : first + width // 16]
@@ -208,15 +230,14 @@ def tile_batchedgraphsagemean1_b_kernel(
                             longer[:], x_f32[b * F_BLOCKS + f][:].indirect(piece), running[f], ALU.add
                         )
                         running[f] = longer[:]
-                agg_bf = [means.tile([P, width], BF16, name="agg_bf") for f in range(F_BLOCKS)]
-                for f in range(F_BLOCKS):
-                    if i1 < len(blocks):
+                        if by_vector and k == NEIGHBOURS - 1 and f > 0:
+                            round_on_vector(f - 1)
+                if by_vector:
+                    round_on_vector(F_BLOCKS - 1)
+                else:
+                    for f in range(F_BLOCKS):
                         nc.scalar.activation(
                             agg_bf[f][:], running[f], FUNC.Copy, scale=1.0 / NEIGHBOURS
-                        )
-                    else:
-                        nc.vector.tensor_scalar(
-                            agg_bf[f][:], running[f], 1.0 / NEIGHBOURS, None, ALU.mult
                         )
 
                 def project_nei(i):
@@ -243,81 +264,89 @@ def tile_batchedgraphsagemean1_b_kernel(
             for i in not_yet_added:
                 add_to_batch_sums(i)
 
-        mean = held.tile([P, Q_BLOCKS], F32, name="mean")
-        square_of_mean = held.tile([P, Q_BLOCKS], F32, name="square_of_mean")
-        eps_less_square = held.tile([P, Q_BLOCKS], F32, name="eps_less_square")
+        count_sum_squares = held.tile([P, Q_BLOCKS], F32, name="count_sum_squares")
+        minus_var = held.tile([P, Q_BLOCKS], F32, name="minus_var")
         minus_mean_gamma = held.tile([P, Q_BLOCKS], F32, name="minus_mean_gamma")
-        mean_of_squares = held.tile([P, Q_BLOCKS], F32, name="mean_of_squares")
         inv_std = held.tile([P, Q_BLOCKS], F32, name="inv_std")
         gain = held.tile([P, Q_BLOCKS], F32, name="gain")
         shift = held.tile([P, Q_BLOCKS], F32, name="shift")
         out_blocks = out.rearrange("(b j p) s -> j p b s", b=GRAPHS, p=P)
         with tc.psum_pool(name="turned_banks", bufs=8 - GRAM_BANKS) as turned_banks:
-            for t in range(GRAM_BANKS):
-                in_bank = min(GRAMS_IN_BANK, Q_BLOCKS - t * GRAMS_IN_BANK)
-                these = slice(t * GRAMS_IN_BANK, t * GRAMS_IN_BANK + in_bank)
-                sums_of_r = grams[t][:, P : P + (in_bank - 1) * R_STEP + 1 : R_STEP]
-                nc.scalar.activation(square_of_mean[:, these], sums_of_r, FUNC.Square, scale=1.0 / COUNT)
-                nc.scalar.activation(mean[:, these], sums_of_r, FUNC.Copy, scale=1.0 / COUNT)
-                for j in range(these.start, these.stop):
-                    column = slice(j, j + 1)
-                    place = (j % GRAMS_IN_BANK) * R_STEP
-                    diagonal = scratch.tile([P, P], F32, name="diagonal")
-                    nc.vector.scalar_tensor_tensor(
-                        out=diagonal[:],
-                        in0=grams[t][:, place : place + P],
-                        scalar=1.0 / COUNT,
-                        in1=ident_f32[:],
-                        op0=ALU.mult,
-                        op1=ALU.mult,
-                        accum_out=mean_of_squares[:, column],
-                    )
-                    if j == these.start:
-                        nc.vector.tensor_scalar(
-                            eps_less_square[:, these], square_of_mean[:, these], -1.0, EPS, ALU.mult, ALU.add
-                        )
-                        nc.vector.scalar_tensor_tensor(
-                            out=minus_mean_gamma[:, these],
-                            in0=mean[:, these],
-                            scalar=-1.0,
-                            in1=gamma_t[:, these],
-                            op0=ALU.mult,
-                            op1=ALU.mult,
-                        )
-                    nc.scalar.activation(
-                        inv_std[:, column],
-                        mean_of_squares[:, column],
-                        FUNC.Abs_reciprocal_sqrt,
-                        bias=eps_less_square[:, column],
-                    )
-                    nc.scalar.activation(
-                        gain[:, column], gamma_t[:, column], FUNC.Copy, scale=inv_std[:, column]
-                    )
-                    nc.scalar.activation(
-                        shift[:, column],
-                        minus_mean_gamma[:, column],
-                        FUNC.Identity,
-                        bias=beta_t[:, column],
-                        scale=inv_std[:, column],
-                    )
 
-                    y = results.tile([P, GRAPHS, NODES], F32, name="y")
-                    for b in range(GRAPHS):
-                        r_turned = turned_banks.tile([P, NODES], BF16, name="r_turned")
-                        for n in range(NODE_BLOCKS):
-                            nc.tensor.transpose(
-                                r_turned[:, n * P : (n + 1) * P], r_tiles[b][n][:, j, 0:P], ident_bf[:]
-                            )
-                        if b == 0:
-                            nc.scalar.activation(
-                                y[:, b, :],
-                                r_turned[:],
-                                FUNC.Identity,
-                                bias=shift[:, column],
-                                scale=gain[:, column],
-                            )
-                        else:
-                            nc.vector.tensor_scalar(
-                                y[:, b, :], r_turned[:], gain[:, column], shift[:, column], ALU.mult, ALU.add
-                            )
-                    nc.sync.dma_start(out_blocks[j], y[:])
+            def gain_and_shift(j):
+                column = slice(j, j + 1)
+                sum_of_r = gram_of[j][:, P : P + 1]
+                diagonal = scratch.tile([P, P], F32, name="diagonal")
+                nc.vector.scalar_tensor_tensor(
+                    out=diagonal[:],
+                    in0=gram_of[j][:, 0:P],
+                    scalar=float(COUNT),
+                    in1=ident_f32[:],
+                    op0=ALU.mult,
+                    op1=ALU.mult,
+                    accum_out=count_sum_squares[:, column],
+                )
+                nc.vector.scalar_tensor_tensor(
+                    out=minus_var[:, column],
+                    in0=sum_of_r,
+                    scalar=sum_of_r,
+                    in1=count_sum_squares[:, column],
+                    op0=ALU.mult,
+                    op1=ALU.subtract,
+                )
+                nc.vector.scalar_tensor_tensor(
+                    out=minus_mean_gamma[:, column],
+                    in0=sum_of_r,
+                    scalar=-1.0 / COUNT,
+                    in1=gamma_t[:, column],
+                    op0=ALU.mult,
+                    op1=ALU.mult,
+                )
+                nc.scalar.activation(
+                    inv_std[:, column],
+                    minus_var[:, column],
+                    FUNC.Abs_reciprocal_sqrt,
+                    bias=EPS,
+                    scale=-1.0 / (COUNT * COUNT),
+                )
+                nc.scalar.activation(
+                    gain[:, column], gamma_t[:, column], FUNC.Copy, scale=inv_std[:, column]
+                )
+                nc.scalar.activation(
+                    shift[:, column],
+                    minus_mean_gamma[:, column],
+                    FUNC.Identity,
+                    bias=beta_t[:, column],
+                    scale=inv_std[:, column],
+                )
+
+            def write_out(j):
+                column = slice(j, j + 1)
+                y = results.tile([P, GRAPHS, NODES], F32, name="y")
+                turned = []
+                for b in range(GRAPHS):
+                    r_turned = turned_banks.tile([P, NODES], BF16, name="r_turned")
+                    for n in range(NODE_BLOCKS):
+                        nc.tensor.transpose(
+                            r_turned[:, n * P : (n + 1) * P], r_tiles[b][n][:, j, 0:P], ident_bf[:]
+                        )
+                    turned.append(r_turned)
+                halves = 2 if j == 0 else 1
+                for nodes in [slice(a * NODES // halves, (a + 1) * NODES // halves) for a in range(halves)]:
+                    nc.scalar.activation(
+                        y[:, 0, nodes],
+                        turned[0][:, nodes],
+                        FUNC.Identity,
+                        bias=shift[:, column],
+                        scale=gain[:, column],
+                    )
+                    nc.vector.tensor_scalar(
+                        y[:, 1, nodes], turned[1][:, nodes], gain[:, column], shift[:, column], ALU.mult, ALU.add
+                    )
+                    nc.sync.dma_start(out_blocks[j][:, :, nodes], y[:, :, nodes])
+
+            gain_and_shift(0)
+            for j in range(Q_BLOCKS):
+                if j + 1 < Q_BLOCKS:
+                    gain_and_shift(j + 1)
+                write_out(j)

@@ -44,8 +44,9 @@ def tile_batchedgraphsagemean1_b_kernel(
         tc.tile_pool(name="means", bufs=F_BLOCKS) as means,
         tc.tile_pool(name="small", bufs=3 * GROUP) as small,
         tc.tile_pool(name="scratch", bufs=2) as scratch,
-        tc.tile_pool(name="results", bufs=4) as results,
+        tc.tile_pool(name="results", bufs=5) as results,
         tc.psum_pool(name="gram_banks", bufs=1) as gram_banks,
+        tc.psum_pool(name="h_banks", bufs=GROUP) as h_banks,
     ):
         lists = held.tile([P, NEIGHBOURS * NODES // 16], U16, name="lists")
         nc.sync.dma_start(lists[:], offs)
@@ -113,156 +114,155 @@ def tile_batchedgraphsagemean1_b_kernel(
         first_rounded_by_vector = len(pieces) - ROUNDED_BY_VECTOR
         blocks = [(b, n) for b, c0, width in pieces for n in range(c0 // P, (c0 + width) // P)]
 
-        with tc.psum_pool(name="h_banks", bufs=GROUP) as h_banks:
 
-            def project(part, half, nodes_of):
-                h_half = h_banks.tile([P, F_OUT], F32, name=f"h_{part}", bufs=H_BUFS[part])
+        def project(part, half, nodes_of):
+            h_half = h_banks.tile([P, F_OUT], F32, name=f"h_{part}", bufs=H_BUFS[part])
+            nc.tensor.matmul(
+                h_half[:],
+                lhsT=first_row[:],
+                rhs=bias_rows[:, half * F_OUT : (half + 1) * F_OUT],
+                start=True,
+                stop=False,
+            )
+            for f in range(F_BLOCKS):
                 nc.tensor.matmul(
                     h_half[:],
-                    lhsT=first_row[:],
-                    rhs=bias_rows[:, half * F_OUT : (half + 1) * F_OUT],
-                    start=True,
-                    stop=False,
+                    lhsT=nodes_of[f],
+                    rhs=weights[part][:, f, :],
+                    start=False,
+                    stop=(f == F_BLOCKS - 1),
                 )
-                for f in range(F_BLOCKS):
-                    nc.tensor.matmul(
-                        h_half[:],
-                        lhsT=nodes_of[f],
-                        rhs=weights[part][:, f, :],
-                        start=False,
-                        stop=(f == F_BLOCKS - 1),
-                    )
-                return h_half
+            return h_half
 
-            def sum_of_squares(h_half, total):
-                squares = scratch.tile([P, F_OUT], BF16, name="squares")
-                nc.scalar.activation(squares[:], h_half[:], FUNC.Square, accum_out=total)
+        def sum_of_squares(h_half, total):
+            squares = scratch.tile([P, F_OUT], BF16, name="squares")
+            nc.scalar.activation(squares[:], h_half[:], FUNC.Square, accum_out=total)
 
-            h_self, h_nei, square_sums = {}, {}, {}
-            self_squared = []
-            not_yet_added = []
+        h_self, h_nei, square_sums = {}, {}, {}
+        self_squared = []
+        not_yet_added = []
 
-            def project_self(i):
-                b, n = blocks[i]
-                in_x = slice(n * P, (n + 1) * P)
-                h_self[i] = project("self", 0, [x_bf[b * F_BLOCKS + f][:, in_x] for f in range(F_BLOCKS)])
-                square_sums[i] = small.tile([P, 2], F32, name="square_sums")
+        def project_self(i):
+            b, n = blocks[i]
+            in_x = slice(n * P, (n + 1) * P)
+            h_self[i] = project("self", 0, [x_bf[b * F_BLOCKS + f][:, in_x] for f in range(F_BLOCKS)])
+            square_sums[i] = small.tile([P, 2], F32, name="square_sums")
 
-            def square_self_up_to(last):
-                for i in range(len(self_squared), last + 1):
-                    sum_of_squares(h_self[i], square_sums[i][:, 0:1])
-                    self_squared.append(i)
+        def square_self_up_to(last):
+            for i in range(len(self_squared), last + 1):
+                sum_of_squares(h_self[i], square_sums[i][:, 0:1])
+                self_squared.append(i)
 
-            def normalise(i):
-                inv_norm = small.tile([P, 1], F32, name="inv_norm")
+        def normalise(i):
+            inv_norm = small.tile([P, 1], F32, name="inv_norm")
+            nc.scalar.activation(
+                inv_norm[:],
+                square_sums[i][:, 0:1],
+                FUNC.Abs_reciprocal_sqrt,
+                bias=square_sums[i][:, 1:2],
+            )
+            b, n = blocks[i]
+            r = r_tiles[b][n]
+            first_bank = len(BLOCKS_OF_GRAM_BANK[0])
+            steps = ((0, HALF_BLOCKS),) if i < len(blocks) - 1 else ((0, first_bank), (first_bank, HALF_BLOCKS))
+            for j0, j1 in steps:
                 nc.scalar.activation(
-                    inv_norm[:],
-                    square_sums[i][:, 0:1],
-                    FUNC.Abs_reciprocal_sqrt,
-                    bias=square_sums[i][:, 1:2],
+                    r[:, j0:j1, 0:P],
+                    h_self[i][:, j0 * P : j1 * P].rearrange("p (j c) -> p j c", c=P),
+                    FUNC.Relu,
+                    scale=inv_norm[:, 0:1],
                 )
-                b, n = blocks[i]
-                r = r_tiles[b][n]
-                first_bank = len(BLOCKS_OF_GRAM_BANK[0])
-                steps = ((0, HALF_BLOCKS),) if i < len(blocks) - 1 else ((0, first_bank), (first_bank, HALF_BLOCKS))
-                for j0, j1 in steps:
+            if i < len(blocks) - last_piece_blocks:
+                nc.scalar.activation(
+                    r[:, HALF_BLOCKS:Q_BLOCKS, 0:P],
+                    h_nei[i][:].rearrange("p (j c) -> p j c", c=P),
+                    FUNC.Relu,
+                    scale=inv_norm[:, 0:1],
+                )
+            else:
+                nc.vector.tensor_scalar(
+                    r[:, HALF_BLOCKS:Q_BLOCKS, 0:P],
+                    h_nei[i][:].rearrange("p (j c) -> p j c", c=P),
+                    inv_norm[:, 0:1],
+                    0.0,
+                    ALU.mult,
+                    ALU.max,
+                )
+
+        def add_to_batch_sums(i):
+            b, n = blocks[i]
+            r = r_tiles[b][n]
+            for j in range(Q_BLOCKS):
+                in_bank = BLOCKS_OF_GRAM_BANK[gram_bank_of[j]]
+                nc.tensor.matmul(
+                    gram_of[j],
+                    lhsT=r[:, j, 0:P],
+                    rhs=r[:, j, 0 : P + 1],
+                    start=(i == 0 and j == in_bank[0]),
+                    stop=(i == len(blocks) - 1 and j == in_bank[-1]),
+                )
+
+        for i in range(GROUP):
+            project_self(i)
+        square_self_up_to(GROUP - 1)
+
+        i1 = 0
+        for t, (b, c0, width) in enumerate(pieces):
+            i0, i1 = i1, i1 + width // P
+            by_vector = t >= first_rounded_by_vector
+            if by_vector:
+                agg_bf = [
+                    held.tile([P, width], BF16, name=f"agg_bf_{t}_{f}") for f in range(F_BLOCKS)
+                ]
+            else:
+                agg_bf = [means.tile([P, width], BF16, name="agg_bf") for f in range(F_BLOCKS)]
+            running = [zeros[:, 0:width] for f in range(F_BLOCKS)]
+
+            def round_on_vector(f):
+                nc.vector.tensor_scalar(agg_bf[f][:], running[f], 1.0 / NEIGHBOURS, None, ALU.mult)
+
+            for k in range(NEIGHBOURS):
+                first = (k * NODES + c0) // 16
+                piece = lists[:, first : first + width // 16]
+                for f in range(F_BLOCKS):
+                    longer = sums.tile([P, width], F32, name="running_sum")
+                    nc.vector.tensor_tensor(
+                        longer[:], x_f32[b * F_BLOCKS + f][:].indirect(piece), running[f], ALU.add
+                    )
+                    running[f] = longer[:]
+                    if by_vector and k == NEIGHBOURS - 1 and f > 0:
+                        round_on_vector(f - 1)
+            if by_vector:
+                round_on_vector(F_BLOCKS - 1)
+            else:
+                for f in range(F_BLOCKS):
                     nc.scalar.activation(
-                        r[:, j0:j1, 0:P],
-                        h_self[i][:, j0 * P : j1 * P].rearrange("p (j c) -> p j c", c=P),
-                        FUNC.Relu,
-                        scale=inv_norm[:, 0:1],
-                    )
-                if i < len(blocks) - last_piece_blocks:
-                    nc.scalar.activation(
-                        r[:, HALF_BLOCKS:Q_BLOCKS, 0:P],
-                        h_nei[i][:].rearrange("p (j c) -> p j c", c=P),
-                        FUNC.Relu,
-                        scale=inv_norm[:, 0:1],
-                    )
-                else:
-                    nc.vector.tensor_scalar(
-                        r[:, HALF_BLOCKS:Q_BLOCKS, 0:P],
-                        h_nei[i][:].rearrange("p (j c) -> p j c", c=P),
-                        inv_norm[:, 0:1],
-                        0.0,
-                        ALU.mult,
-                        ALU.max,
+                        agg_bf[f][:], running[f], FUNC.Copy, scale=1.0 / NEIGHBOURS
                     )
 
-            def add_to_batch_sums(i):
-                b, n = blocks[i]
-                r = r_tiles[b][n]
-                for j in range(Q_BLOCKS):
-                    in_bank = BLOCKS_OF_GRAM_BANK[gram_bank_of[j]]
-                    nc.tensor.matmul(
-                        gram_of[j],
-                        lhsT=r[:, j, 0:P],
-                        rhs=r[:, j, 0 : P + 1],
-                        start=(i == 0 and j == in_bank[0]),
-                        stop=(i == len(blocks) - 1 and j == in_bank[-1]),
-                    )
+            def project_nei(i):
+                in_piece = slice((i - i0) * P, (i - i0 + 1) * P)
+                h_nei[i] = project("nei", 1, [agg_bf[f][:, in_piece] for f in range(F_BLOCKS)])
 
-            for i in range(GROUP):
-                project_self(i)
-            square_self_up_to(GROUP - 1)
-
-            i1 = 0
-            for t, (b, c0, width) in enumerate(pieces):
-                i0, i1 = i1, i1 + width // P
-                by_vector = t >= first_rounded_by_vector
-                if by_vector:
-                    agg_bf = [
-                        held.tile([P, width], BF16, name=f"agg_bf_{t}_{f}") for f in range(F_BLOCKS)
-                    ]
-                else:
-                    agg_bf = [means.tile([P, width], BF16, name="agg_bf") for f in range(F_BLOCKS)]
-                running = [zeros[:, 0:width] for f in range(F_BLOCKS)]
-
-                def round_on_vector(f):
-                    nc.vector.tensor_scalar(agg_bf[f][:], running[f], 1.0 / NEIGHBOURS, None, ALU.mult)
-
-                for k in range(NEIGHBOURS):
-                    first = (k * NODES + c0) // 16
-                    piece = lists[:, first : first + width // 16]
-                    for f in range(F_BLOCKS):
-                        longer = sums.tile([P, width], F32, name="running_sum")
-                        nc.vector.tensor_tensor(
-                            longer[:], x_f32[b * F_BLOCKS + f][:].indirect(piece), running[f], ALU.add
-                        )
-                        running[f] = longer[:]
-                        if by_vector and k == NEIGHBOURS - 1 and f > 0:
-                            round_on_vector(f - 1)
-                if by_vector:
-                    round_on_vector(F_BLOCKS - 1)
-                else:
-                    for f in range(F_BLOCKS):
-                        nc.scalar.activation(
-                            agg_bf[f][:], running[f], FUNC.Copy, scale=1.0 / NEIGHBOURS
-                        )
-
-                def project_nei(i):
-                    in_piece = slice((i - i0) * P, (i - i0 + 1) * P)
-                    h_nei[i] = project("nei", 1, [agg_bf[f][:, in_piece] for f in range(F_BLOCKS)])
-
-                for i in range(i0, min(i0 + GROUP, i1)):
-                    project_nei(i)
-                for i in not_yet_added:
-                    add_to_batch_sums(i)
-                not_yet_added.clear()
-                for i in range(i0, i1):
-                    square_self_up_to(i)
-                    sum_of_squares(h_nei[i], square_sums[i][:, 1:2])
-                    normalise(i)
-                    if i + GROUP < len(blocks):
-                        project_self(i + GROUP)
-                    if i + GROUP < i1:
-                        project_nei(i + GROUP)
-                        add_to_batch_sums(i)
-                    else:
-                        not_yet_added.append(i)
-                square_self_up_to(min(i1 + GROUP, len(blocks)) - 1)
+            for i in range(i0, min(i0 + GROUP, i1)):
+                project_nei(i)
             for i in not_yet_added:
                 add_to_batch_sums(i)
+            not_yet_added.clear()
+            for i in range(i0, i1):
+                square_self_up_to(i)
+                sum_of_squares(h_nei[i], square_sums[i][:, 1:2])
+                normalise(i)
+                if i + GROUP < len(blocks):
+                    project_self(i + GROUP)
+                if i + GROUP < i1:
+                    project_nei(i + GROUP)
+                    add_to_batch_sums(i)
+                else:
+                    not_yet_added.append(i)
+            square_self_up_to(min(i1 + GROUP, len(blocks)) - 1)
+        for i in not_yet_added:
+            add_to_batch_sums(i)
 
         count_sum_squares = held.tile([P, Q_BLOCKS], F32, name="count_sum_squares")
         minus_var = held.tile([P, Q_BLOCKS], F32, name="minus_var")
@@ -271,82 +271,84 @@ def tile_batchedgraphsagemean1_b_kernel(
         gain = held.tile([P, Q_BLOCKS], F32, name="gain")
         shift = held.tile([P, Q_BLOCKS], F32, name="shift")
         out_blocks = out.rearrange("(b j p) s -> j p b s", b=GRAPHS, p=P)
-        with tc.psum_pool(name="turned_banks", bufs=8 - GRAM_BANKS) as turned_banks:
 
-            def gain_and_shift(j):
-                column = slice(j, j + 1)
-                sum_of_r = gram_of[j][:, P : P + 1]
-                diagonal = scratch.tile([P, P], F32, name="diagonal")
-                nc.vector.scalar_tensor_tensor(
-                    out=diagonal[:],
-                    in0=gram_of[j][:, 0:P],
-                    scalar=float(COUNT),
-                    in1=ident_f32[:],
-                    op0=ALU.mult,
-                    op1=ALU.mult,
-                    accum_out=count_sum_squares[:, column],
+        def gain_and_shift(j):
+            column = slice(j, j + 1)
+            sum_of_r = gram_of[j][:, P : P + 1]
+            diagonal = scratch.tile([P, P], F32, name="diagonal")
+            nc.vector.scalar_tensor_tensor(
+                out=diagonal[:],
+                in0=gram_of[j][:, 0:P],
+                scalar=float(COUNT),
+                in1=ident_f32[:],
+                op0=ALU.mult,
+                op1=ALU.mult,
+                accum_out=count_sum_squares[:, column],
+            )
+            nc.vector.scalar_tensor_tensor(
+                out=minus_var[:, column],
+                in0=sum_of_r,
+                scalar=sum_of_r,
+                in1=count_sum_squares[:, column],
+                op0=ALU.mult,
+                op1=ALU.subtract,
+            )
+            nc.vector.scalar_tensor_tensor(
+                out=minus_mean_gamma[:, column],
+                in0=sum_of_r,
+                scalar=-1.0 / COUNT,
+                in1=gamma_t[:, column],
+                op0=ALU.mult,
+                op1=ALU.mult,
+            )
+            nc.scalar.activation(
+                inv_std[:, column],
+                minus_var[:, column],
+                FUNC.Abs_reciprocal_sqrt,
+                bias=EPS,
+                scale=-1.0 / (COUNT * COUNT),
+            )
+            nc.scalar.activation(
+                gain[:, column], gamma_t[:, column], FUNC.Copy, scale=inv_std[:, column]
+            )
+            nc.scalar.activation(
+                shift[:, column],
+                minus_mean_gamma[:, column],
+                FUNC.Identity,
+                bias=beta_t[:, column],
+                scale=inv_std[:, column],
+            )
+
+        def write_out(j):
+            column = slice(j, j + 1)
+            y = results.tile([P, GRAPHS, NODES], F32, name="y")
+            turned = []
+            for b in range(GRAPHS):
+                part = ("nei", "self")[b]
+                r_turned = h_banks.tile(
+                    [P, NODES], BF16, name="r_turned", tag=f"h_{part}", bufs=H_BUFS[part]
                 )
-                nc.vector.scalar_tensor_tensor(
-                    out=minus_var[:, column],
-                    in0=sum_of_r,
-                    scalar=sum_of_r,
-                    in1=count_sum_squares[:, column],
-                    op0=ALU.mult,
-                    op1=ALU.subtract,
-                )
-                nc.vector.scalar_tensor_tensor(
-                    out=minus_mean_gamma[:, column],
-                    in0=sum_of_r,
-                    scalar=-1.0 / COUNT,
-                    in1=gamma_t[:, column],
-                    op0=ALU.mult,
-                    op1=ALU.mult,
-                )
+                for n in range(NODE_BLOCKS):
+                    nc.tensor.transpose(
+                        r_turned[:, n * P : (n + 1) * P], r_tiles[b][n][:, j, 0:P], ident_bf[:]
+                    )
+                turned.append(r_turned)
+            halves = 2 if j == 0 else 1
+            for nodes in [slice(a * NODES // halves, (a + 1) * NODES // halves) for a in range(halves)]:
                 nc.scalar.activation(
-                    inv_std[:, column],
-                    minus_var[:, column],
-                    FUNC.Abs_reciprocal_sqrt,
-                    bias=EPS,
-                    scale=-1.0 / (COUNT * COUNT),
-                )
-                nc.scalar.activation(
-                    gain[:, column], gamma_t[:, column], FUNC.Copy, scale=inv_std[:, column]
-                )
-                nc.scalar.activation(
-                    shift[:, column],
-                    minus_mean_gamma[:, column],
+                    y[:, 0, nodes],
+                    turned[0][:, nodes],
                     FUNC.Identity,
-                    bias=beta_t[:, column],
-                    scale=inv_std[:, column],
+                    bias=shift[:, column],
+                    scale=gain[:, column],
                 )
+                nc.vector.tensor_scalar(
+                    y[:, 1, nodes], turned[1][:, nodes], gain[:, column], shift[:, column], ALU.mult, ALU.add
+                )
+                nc.sync.dma_start(out_blocks[j][:, :, nodes], y[:, :, nodes])
 
-            def write_out(j):
-                column = slice(j, j + 1)
-                y = results.tile([P, GRAPHS, NODES], F32, name="y")
-                turned = []
-                for b in range(GRAPHS):
-                    r_turned = turned_banks.tile([P, NODES], BF16, name="r_turned")
-                    for n in range(NODE_BLOCKS):
-                        nc.tensor.transpose(
-                            r_turned[:, n * P : (n + 1) * P], r_tiles[b][n][:, j, 0:P], ident_bf[:]
-                        )
-                    turned.append(r_turned)
-                halves = 2 if j == 0 else 1
-                for nodes in [slice(a * NODES // halves, (a + 1) * NODES // halves) for a in range(halves)]:
-                    nc.scalar.activation(
-                        y[:, 0, nodes],
-                        turned[0][:, nodes],
-                        FUNC.Identity,
-                        bias=shift[:, column],
-                        scale=gain[:, column],
-                    )
-                    nc.vector.tensor_scalar(
-                        y[:, 1, nodes], turned[1][:, nodes], gain[:, column], shift[:, column], ALU.mult, ALU.add
-                    )
-                    nc.sync.dma_start(out_blocks[j][:, :, nodes], y[:, :, nodes])
-
-            gain_and_shift(0)
-            for j in range(Q_BLOCKS):
-                if j + 1 < Q_BLOCKS:
-                    gain_and_shift(j + 1)
-                write_out(j)
+        gain_and_shift(0)
+        for j in range(Q_BLOCKS):
+            if j + 1 < Q_BLOCKS:
+                gain_and_shift(j + 1)
+            write_out(j)

@@ -18,18 +18,20 @@ F_BLOCKS = F_IN // P
 Q_BLOCKS = CHANNELS // P
 NODE_BLOCKS = NODES // P
 HALF_BLOCKS = F_OUT // P
-PIECE_WIDTHS = ((512, 512), (384, 256, 256, 128))
-WIDEST = 512
-ROUNDED_BY_VECTOR = 2
-GROUP = 2
-H_BUFS = {"self": 2, "nei": 3}
 COUNT = GRAPHS * NODES
 EPS = 1e-5
 
+PIECE_WIDTHS = ((512, 512), (384, 256, 256, 128))
+WIDEST = 512
+ROUNDED_BY_VECTOR = 2
+
+AHEAD = 2
+H_BANKS = {"self": 2, "nei": 2}
+
 R_STEP = P + 2
-GRAMS_IN_BANK = 3
-BLOCKS_OF_GRAM_BANK = ((0, 1), (2, 3, 4), (5, 6, 7))
-GRAM_BANKS = len(BLOCKS_OF_GRAM_BANK)
+MOST_IN_BANK = 3
+BLOCKS_OF_SUM_BANK = ((0,), (1, 2, 3), (4, 5, 6), (7,))
+SUM_BANKS = len(BLOCKS_OF_SUM_BANK)
 
 FLOPS = 2 * GRAPHS * NODES * F_IN * CHANNELS
 
@@ -42,24 +44,24 @@ def tile_batchedgraphsagemean1_b_kernel(
         tc.tile_pool(name="held", bufs=1) as held,
         tc.tile_pool(name="sums", bufs=5 * F_BLOCKS) as sums,
         tc.tile_pool(name="means", bufs=F_BLOCKS) as means,
-        tc.tile_pool(name="small", bufs=3 * GROUP) as small,
+        tc.tile_pool(name="small", bufs=3 * AHEAD) as small,
         tc.tile_pool(name="scratch", bufs=2) as scratch,
         tc.tile_pool(name="results", bufs=5) as results,
-        tc.psum_pool(name="gram_banks", bufs=1) as gram_banks,
-        tc.psum_pool(name="h_banks", bufs=GROUP) as h_banks,
+        tc.psum_pool(name="gram_banks", bufs=1) as sum_banks,
+        tc.psum_pool(name="h_banks", bufs=AHEAD) as h_banks,
     ):
         lists = held.tile([P, NEIGHBOURS * NODES // 16], U16, name="lists")
         nc.sync.dma_start(lists[:], offs)
-        x_f32 = [held.tile([P, NODES], F32, name=f"x_f32_{i}") for i in range(GRAPHS * F_BLOCKS)]
+        x_f32 = [held.tile([P, NODES], F32, name=f"x_f32_{a}") for a in range(GRAPHS * F_BLOCKS)]
         load_queues = (nc.scalar, nc.sync)
-        for i in range(F_BLOCKS):
-            load_queues[i % 2].dma_start(x_f32[i][:], x[i * P : (i + 1) * P, :])
+        for a in range(F_BLOCKS):
+            load_queues[a % 2].dma_start(x_f32[a][:], x[a * P : (a + 1) * P, :])
         weights = {}
-        for part, w in (("self", w_self), ("nei", w_nei)):
-            weights[part] = held.tile([P, F_BLOCKS, F_OUT], BF16, name=f"w_{part}")
-            nc.sync.dma_start(weights[part][:], w.rearrange("(a p) q -> p a q", p=P))
-        for i in range(F_BLOCKS, GRAPHS * F_BLOCKS):
-            nc.sync.dma_start(x_f32[i][:], x[i * P : (i + 1) * P, :])
+        for half_name, w in (("self", w_self), ("nei", w_nei)):
+            weights[half_name] = held.tile([P, F_BLOCKS, F_OUT], BF16, name=f"w_{half_name}")
+            nc.sync.dma_start(weights[half_name][:], w.rearrange("(a p) q -> p a q", p=P))
+        for a in range(F_BLOCKS, GRAPHS * F_BLOCKS):
+            nc.sync.dma_start(x_f32[a][:], x[a * P : (a + 1) * P, :])
 
         bias_f32 = held.tile([1, CHANNELS], F32, name="bias_f32")
         nc.scalar.dma_start(bias_f32[:, 0:F_OUT], bias_self.rearrange("q o -> o q"))
@@ -90,33 +92,32 @@ def tile_batchedgraphsagemean1_b_kernel(
             for n in range(NODE_BLOCKS):
                 nc.vector.memset(r_tiles[b][n][:, :, P : P + 1], 1.0)
 
-        x_bf = [held.tile([P, NODES], BF16, name=f"x_bf_{i}") for i in range(GRAPHS * F_BLOCKS)]
-        for i in range(GRAPHS * F_BLOCKS):
-            nc.scalar.copy(x_bf[i][:], x_f32[i][:])
+        x_bf = [held.tile([P, NODES], BF16, name=f"x_bf_{a}") for a in range(GRAPHS * F_BLOCKS)]
+        for a in range(GRAPHS * F_BLOCKS):
+            nc.scalar.copy(x_bf[a][:], x_f32[a][:])
 
-        grams = [
-            gram_banks.tile([P, GRAMS_IN_BANK * R_STEP], F32, name=f"gram_{t}")
-            for t in range(GRAM_BANKS)
+        sum_tiles = [
+            sum_banks.tile([P, MOST_IN_BANK * R_STEP], F32, name=f"gram_{bank}")
+            for bank in range(SUM_BANKS)
         ]
-        gram_bank_of = {j: t for t in range(GRAM_BANKS) for j in BLOCKS_OF_GRAM_BANK[t]}
-        gram_of = {
-            j: grams[t][:, a * R_STEP : a * R_STEP + P + 1]
-            for t in range(GRAM_BANKS)
-            for a, j in enumerate(BLOCKS_OF_GRAM_BANK[t])
+        sum_bank_of = {j: bank for bank in range(SUM_BANKS) for j in BLOCKS_OF_SUM_BANK[bank]}
+        batch_sums = {
+            j: sum_tiles[bank][:, place * R_STEP : place * R_STEP + P + 1]
+            for bank in range(SUM_BANKS)
+            for place, j in enumerate(BLOCKS_OF_SUM_BANK[bank])
         }
 
         pieces = [
-            (b, sum(PIECE_WIDTHS[b][:t]), width)
+            (b, sum(PIECE_WIDTHS[b][:earlier]), width)
             for b in range(GRAPHS)
-            for t, width in enumerate(PIECE_WIDTHS[b])
+            for earlier, width in enumerate(PIECE_WIDTHS[b])
         ]
         last_piece_blocks = pieces[-1][2] // P
         first_rounded_by_vector = len(pieces) - ROUNDED_BY_VECTOR
         blocks = [(b, n) for b, c0, width in pieces for n in range(c0 // P, (c0 + width) // P)]
 
-
-        def project(part, half, nodes_of):
-            h_half = h_banks.tile([P, F_OUT], F32, name=f"h_{part}", bufs=H_BUFS[part])
+        def project(half_name, half, nodes_of):
+            h_half = h_banks.tile([P, F_OUT], F32, name=f"h_{half_name}", bufs=H_BANKS[half_name])
             nc.tensor.matmul(
                 h_half[:],
                 lhsT=first_row[:],
@@ -128,7 +129,7 @@ def tile_batchedgraphsagemean1_b_kernel(
                 nc.tensor.matmul(
                     h_half[:],
                     lhsT=nodes_of[f],
-                    rhs=weights[part][:, f, :],
+                    rhs=weights[half_name][:, f, :],
                     start=False,
                     stop=(f == F_BLOCKS - 1),
                 )
@@ -163,8 +164,11 @@ def tile_batchedgraphsagemean1_b_kernel(
             )
             b, n = blocks[i]
             r = r_tiles[b][n]
-            first_bank = len(BLOCKS_OF_GRAM_BANK[0])
-            steps = ((0, HALF_BLOCKS),) if i < len(blocks) - 1 else ((0, first_bank), (first_bank, HALF_BLOCKS))
+            in_first_bank = len(BLOCKS_OF_SUM_BANK[0])
+            if i < len(blocks) - 1:
+                steps = ((0, HALF_BLOCKS),)
+            else:
+                steps = ((0, in_first_bank), (in_first_bank, HALF_BLOCKS))
             for j0, j1 in steps:
                 nc.scalar.activation(
                     r[:, j0:j1, 0:P],
@@ -193,18 +197,18 @@ def tile_batchedgraphsagemean1_b_kernel(
             b, n = blocks[i]
             r = r_tiles[b][n]
             for j in range(Q_BLOCKS):
-                in_bank = BLOCKS_OF_GRAM_BANK[gram_bank_of[j]]
+                in_bank = BLOCKS_OF_SUM_BANK[sum_bank_of[j]]
                 nc.tensor.matmul(
-                    gram_of[j],
+                    batch_sums[j],
                     lhsT=r[:, j, 0:P],
                     rhs=r[:, j, 0 : P + 1],
                     start=(i == 0 and j == in_bank[0]),
                     stop=(i == len(blocks) - 1 and j == in_bank[-1]),
                 )
 
-        for i in range(GROUP):
+        for i in range(AHEAD):
             project_self(i)
-        square_self_up_to(GROUP - 1)
+        square_self_up_to(AHEAD - 1)
 
         i1 = 0
         for t, (b, c0, width) in enumerate(pieces):
@@ -222,12 +226,12 @@ def tile_batchedgraphsagemean1_b_kernel(
                 nc.vector.tensor_scalar(agg_bf[f][:], running[f], 1.0 / NEIGHBOURS, None, ALU.mult)
 
             for k in range(NEIGHBOURS):
-                first = (k * NODES + c0) // 16
-                piece = lists[:, first : first + width // 16]
+                first_column = (k * NODES + c0) // 16
+                offsets = lists[:, first_column : first_column + width // 16]
                 for f in range(F_BLOCKS):
                     longer = sums.tile([P, width], F32, name="running_sum")
                     nc.vector.tensor_tensor(
-                        longer[:], x_f32[b * F_BLOCKS + f][:].indirect(piece), running[f], ALU.add
+                        longer[:], x_f32[b * F_BLOCKS + f][:].indirect(offsets), running[f], ALU.add
                     )
                     running[f] = longer[:]
                     if by_vector and k == NEIGHBOURS - 1 and f > 0:
@@ -244,7 +248,7 @@ def tile_batchedgraphsagemean1_b_kernel(
                 in_piece = slice((i - i0) * P, (i - i0 + 1) * P)
                 h_nei[i] = project("nei", 1, [agg_bf[f][:, in_piece] for f in range(F_BLOCKS)])
 
-            for i in range(i0, min(i0 + GROUP, i1)):
+            for i in range(i0, min(i0 + AHEAD, i1)):
                 project_nei(i)
             for i in not_yet_added:
                 add_to_batch_sums(i)
@@ -253,14 +257,14 @@ def tile_batchedgraphsagemean1_b_kernel(
                 square_self_up_to(i)
                 sum_of_squares(h_nei[i], square_sums[i][:, 1:2])
                 normalise(i)
-                if i + GROUP < len(blocks):
-                    project_self(i + GROUP)
-                if i + GROUP < i1:
-                    project_nei(i + GROUP)
+                if i + AHEAD < len(blocks):
+                    project_self(i + AHEAD)
+                if i + AHEAD < i1:
+                    project_nei(i + AHEAD)
                     add_to_batch_sums(i)
                 else:
                     not_yet_added.append(i)
-            square_self_up_to(min(i1 + GROUP, len(blocks)) - 1)
+            square_self_up_to(min(i1 + AHEAD, len(blocks)) - 1)
         for i in not_yet_added:
             add_to_batch_sums(i)
 
@@ -274,11 +278,11 @@ def tile_batchedgraphsagemean1_b_kernel(
 
         def gain_and_shift(j):
             column = slice(j, j + 1)
-            sum_of_r = gram_of[j][:, P : P + 1]
+            sum_of_r = batch_sums[j][:, P : P + 1]
             diagonal = scratch.tile([P, P], F32, name="diagonal")
             nc.vector.scalar_tensor_tensor(
                 out=diagonal[:],
-                in0=gram_of[j][:, 0:P],
+                in0=batch_sums[j][:, 0:P],
                 scalar=float(COUNT),
                 in1=ident_f32[:],
                 op0=ALU.mult,
@@ -324,9 +328,9 @@ def tile_batchedgraphsagemean1_b_kernel(
             y = results.tile([P, GRAPHS, NODES], F32, name="y")
             turned = []
             for b in range(GRAPHS):
-                part = ("nei", "self")[b]
+                ring = ("nei", "self")[b]
                 r_turned = h_banks.tile(
-                    [P, NODES], BF16, name="r_turned", tag=f"h_{part}", bufs=H_BUFS[part]
+                    [P, NODES], BF16, name="r_turned", tag=f"h_{ring}", bufs=H_BANKS[ring]
                 )
                 for n in range(NODE_BLOCKS):
                     nc.tensor.transpose(
@@ -334,7 +338,8 @@ def tile_batchedgraphsagemean1_b_kernel(
                     )
                 turned.append(r_turned)
             halves = 2 if j == 0 else 1
-            for nodes in [slice(a * NODES // halves, (a + 1) * NODES // halves) for a in range(halves)]:
+            for first_node in range(0, NODES, NODES // halves):
+                nodes = slice(first_node, first_node + NODES // halves)
                 nc.scalar.activation(
                     y[:, 0, nodes],
                     turned[0][:, nodes],

@@ -69,20 +69,20 @@ def tile_batchedgraphsagemean1_b_kernel(
         gamma_t = held.tile([P, Q_BLOCKS], F32, name="gamma_t")
         beta_t = held.tile([P, Q_BLOCKS], F32, name="beta_t")
         with nc.allow_non_contiguous_dma(reason="one 4-byte value to a partition, 8 KiB in all"):
-            nc.scalar.dma_start(gamma_t[:], gamma.rearrange("(j p) o -> p (j o)", p=P))
-            nc.scalar.dma_start(beta_t[:], beta.rearrange("(j p) o -> p (j o)", p=P))
+            nc.sync.dma_start(gamma_t[:], gamma.rearrange("(j p) o -> p (j o)", p=P))
+            nc.sync.dma_start(beta_t[:], beta.rearrange("(j p) o -> p (j o)", p=P))
 
         zeros = held.tile([P, WIDEST], F32, name="zeros")
-        nc.gpsimd.memset(zeros[:], 0.0)
+        nc.vector.memset(zeros[:], 0.0)
         ident_bf = held.tile([P, P], BF16, name="ident_bf")
         make_identity(nc, ident_bf[:])
         ident_f32 = held.tile([P, P], F32, name="ident_f32")
         make_identity(nc, ident_f32[:])
         first_row = held.tile([P, P], BF16, name="first_row")
-        nc.gpsimd.memset(first_row[:], 0.0)
-        nc.gpsimd.memset(first_row[0:1, :], 1.0)
+        nc.vector.memset(first_row[:], 0.0)
+        nc.vector.memset(first_row[0:1, :], 1.0)
         bias_rows = held.tile([P, CHANNELS], BF16, name="bias_rows")
-        nc.gpsimd.memset(bias_rows[:], 0.0)
+        nc.vector.memset(bias_rows[:], 0.0)
         nc.scalar.copy(bias_rows[0:1, :], bias_f32[:])
         r_tiles = [
             [held.tile([P, Q_BLOCKS, R_STEP], BF16, name=f"r_{b}_{n}") for n in range(NODE_BLOCKS)]
@@ -193,10 +193,10 @@ def tile_batchedgraphsagemean1_b_kernel(
                     ALU.max,
                 )
 
-        def add_to_batch_sums(i):
+        def add_to_batch_sums(i, channel_blocks=range(Q_BLOCKS)):
             b, n = blocks[i]
             r = r_tiles[b][n]
-            for j in range(Q_BLOCKS):
+            for j in channel_blocks:
                 in_bank = BLOCKS_OF_SUM_BANK[sum_bank_of[j]]
                 nc.tensor.matmul(
                     batch_sums[j],
@@ -265,8 +265,26 @@ def tile_batchedgraphsagemean1_b_kernel(
                 else:
                     not_yet_added.append(i)
             square_self_up_to(min(i1 + AHEAD, len(blocks)) - 1)
+
+        def turn_back(j):
+            turned = []
+            for b in range(GRAPHS):
+                ring = ("nei", "self")[b]
+                r_turned = h_banks.tile(
+                    [P, NODES], BF16, name="r_turned", tag=f"h_{ring}", bufs=H_BANKS[ring]
+                )
+                for n in range(NODE_BLOCKS):
+                    nc.tensor.transpose(
+                        r_turned[:, n * P : (n + 1) * P], r_tiles[b][n][:, j, 0:P], ident_bf[:]
+                    )
+                turned.append(r_turned)
+            return turned
+
         for i in not_yet_added:
-            add_to_batch_sums(i)
+            add_to_batch_sums(i, BLOCKS_OF_SUM_BANK[0])
+        first_turned = turn_back(0)
+        for i in not_yet_added:
+            add_to_batch_sums(i, range(len(BLOCKS_OF_SUM_BANK[0]), Q_BLOCKS))
 
         count_sum_squares = held.tile([P, Q_BLOCKS], F32, name="count_sum_squares")
         minus_var = held.tile([P, Q_BLOCKS], F32, name="minus_var")
@@ -312,9 +330,7 @@ def tile_batchedgraphsagemean1_b_kernel(
                 bias=EPS,
                 scale=-1.0 / (COUNT * COUNT),
             )
-            nc.scalar.activation(
-                gain[:, column], gamma_t[:, column], FUNC.Copy, scale=inv_std[:, column]
-            )
+            nc.vector.tensor_tensor(gain[:, column], gamma_t[:, column], inv_std[:, column], ALU.mult)
             nc.scalar.activation(
                 shift[:, column],
                 minus_mean_gamma[:, column],
@@ -326,17 +342,7 @@ def tile_batchedgraphsagemean1_b_kernel(
         def write_out(j):
             column = slice(j, j + 1)
             y = results.tile([P, GRAPHS, NODES], F32, name="y")
-            turned = []
-            for b in range(GRAPHS):
-                ring = ("nei", "self")[b]
-                r_turned = h_banks.tile(
-                    [P, NODES], BF16, name="r_turned", tag=f"h_{ring}", bufs=H_BANKS[ring]
-                )
-                for n in range(NODE_BLOCKS):
-                    nc.tensor.transpose(
-                        r_turned[:, n * P : (n + 1) * P], r_tiles[b][n][:, j, 0:P], ident_bf[:]
-                    )
-                turned.append(r_turned)
+            turned = first_turned if j == 0 else turn_back(j)
             halves = 2 if j == 0 else 1
             for first_node in range(0, NODES, NODES // halves):
                 nodes = slice(first_node, first_node + NODES // halves)

@@ -62,6 +62,9 @@ def tile_batchedgraphsagemean1_b_kernel(
             nc.sync.dma_start(weights[half_name][:], w.rearrange("(a p) q -> p a q", p=P))
         for a in range(F_BLOCKS, GRAPHS * F_BLOCKS):
             nc.sync.dma_start(x_f32[a][:], x[a * P : (a + 1) * P, :])
+        w_nei_loaded = weights["nei"]
+        weights["nei"] = held.tile([P, F_BLOCKS, F_OUT], BF16, name="w_nei_quarter")
+        nc.scalar.mul(weights["nei"][:], w_nei_loaded[:], 1.0 / NEIGHBOURS)
 
         bias_f32 = held.tile([1, CHANNELS], F32, name="bias_f32")
         nc.scalar.dma_start(bias_f32[:, 0:F_OUT], bias_self.rearrange("q o -> o q"))
@@ -214,16 +217,7 @@ def tile_batchedgraphsagemean1_b_kernel(
         for t, (b, c0, width) in enumerate(pieces):
             i0, i1 = i1, i1 + width // P
             by_vector = t >= first_rounded_by_vector
-            if by_vector:
-                agg_bf = [
-                    held.tile([P, width], BF16, name=f"agg_bf_{t}_{f}") for f in range(F_BLOCKS)
-                ]
-            else:
-                agg_bf = [means.tile([P, width], BF16, name="agg_bf") for f in range(F_BLOCKS)]
             running = [zeros[:, 0:width] for f in range(F_BLOCKS)]
-
-            def round_on_vector(f):
-                nc.vector.tensor_scalar(agg_bf[f][:], running[f], 1.0 / NEIGHBOURS, None, ALU.mult)
 
             for k in range(NEIGHBOURS):
                 first_column = (k * NODES + c0) // 16
@@ -234,15 +228,13 @@ def tile_batchedgraphsagemean1_b_kernel(
                         longer[:], x_f32[b * F_BLOCKS + f][:].indirect(offsets), running[f], ALU.add
                     )
                     running[f] = longer[:]
-                    if by_vector and k == NEIGHBOURS - 1 and f > 0:
-                        round_on_vector(f - 1)
             if by_vector:
-                round_on_vector(F_BLOCKS - 1)
+                agg_bf = [running[f].bitcast(BF16)[:, 1 : 2 * width : 2] for f in range(F_BLOCKS)]
             else:
+                agg_tiles = [means.tile([P, width], BF16, name="agg_bf") for f in range(F_BLOCKS)]
                 for f in range(F_BLOCKS):
-                    nc.scalar.activation(
-                        agg_bf[f][:], running[f], FUNC.Copy, scale=1.0 / NEIGHBOURS
-                    )
+                    nc.scalar.copy(agg_tiles[f][:], running[f])
+                agg_bf = [agg_tiles[f][:] for f in range(F_BLOCKS)]
 
             def project_nei(i):
                 in_piece = slice((i - i0) * P, (i - i0 + 1) * P)

@@ -23,7 +23,6 @@ EPS = 1e-5
 
 PIECE_WIDTHS = ((512, 512), (384, 256, 256, 128))
 WIDEST = 512
-ROUNDED_BY_VECTOR = 2
 
 AHEAD = 2
 H_BANKS = {"self": 2, "nei": 2}
@@ -43,7 +42,6 @@ def tile_batchedgraphsagemean1_b_kernel(
     with (
         tc.tile_pool(name="held", bufs=1) as held,
         tc.tile_pool(name="sums", bufs=5 * F_BLOCKS) as sums,
-        tc.tile_pool(name="means", bufs=F_BLOCKS) as means,
         tc.tile_pool(name="small", bufs=3 * AHEAD) as small,
         tc.tile_pool(name="scratch", bufs=2) as scratch,
         tc.tile_pool(name="results", bufs=5) as results,
@@ -95,9 +93,10 @@ def tile_batchedgraphsagemean1_b_kernel(
             for n in range(NODE_BLOCKS):
                 nc.vector.memset(r_tiles[b][n][:, :, P : P + 1], 1.0)
 
-        x_bf = [held.tile([P, NODES], BF16, name=f"x_bf_{a}") for a in range(GRAPHS * F_BLOCKS)]
-        for a in range(GRAPHS * F_BLOCKS):
-            nc.scalar.copy(x_bf[a][:], x_f32[a][:])
+        def cut_to_bf16(values, columns):
+            return values.bitcast(BF16)[:, 1 : 2 * columns : 2]
+
+        x_bf = [cut_to_bf16(x_f32[a][:], NODES) for a in range(GRAPHS * F_BLOCKS)]
 
         sum_tiles = [
             sum_banks.tile([P, MOST_IN_BANK * R_STEP], F32, name=f"gram_{bank}")
@@ -116,7 +115,6 @@ def tile_batchedgraphsagemean1_b_kernel(
             for earlier, width in enumerate(PIECE_WIDTHS[b])
         ]
         last_piece_blocks = pieces[-1][2] // P
-        first_rounded_by_vector = len(pieces) - ROUNDED_BY_VECTOR
         blocks = [(b, n) for b, c0, width in pieces for n in range(c0 // P, (c0 + width) // P)]
 
         def project(half_name, half, nodes_of):
@@ -216,7 +214,6 @@ def tile_batchedgraphsagemean1_b_kernel(
         i1 = 0
         for t, (b, c0, width) in enumerate(pieces):
             i0, i1 = i1, i1 + width // P
-            by_vector = t >= first_rounded_by_vector
             running = [zeros[:, 0:width] for f in range(F_BLOCKS)]
 
             for k in range(NEIGHBOURS):
@@ -228,18 +225,16 @@ def tile_batchedgraphsagemean1_b_kernel(
                         longer[:], x_f32[b * F_BLOCKS + f][:].indirect(offsets), running[f], ALU.add
                     )
                     running[f] = longer[:]
-            if by_vector:
-                agg_bf = [running[f].bitcast(BF16)[:, 1 : 2 * width : 2] for f in range(F_BLOCKS)]
-            else:
-                agg_tiles = [means.tile([P, width], BF16, name="agg_bf") for f in range(F_BLOCKS)]
-                for f in range(F_BLOCKS):
-                    nc.scalar.copy(agg_tiles[f][:], running[f])
-                agg_bf = [agg_tiles[f][:] for f in range(F_BLOCKS)]
+            agg_bf = [cut_to_bf16(running[f], width) for f in range(F_BLOCKS)]
 
             def project_nei(i):
                 in_piece = slice((i - i0) * P, (i - i0 + 1) * P)
                 h_nei[i] = project("nei", 1, [agg_bf[f][:, in_piece] for f in range(F_BLOCKS)])
 
+            if t < len(pieces) - 1:
+                for i in not_yet_added:
+                    add_to_batch_sums(i)
+                not_yet_added.clear()
             for i in range(i0, min(i0 + AHEAD, i1)):
                 project_nei(i)
             for i in not_yet_added:

@@ -237,9 +237,6 @@ def tile_batchedgraphsagemean1_b_kernel(
                 not_yet_added.clear()
             for i in range(i0, min(i0 + AHEAD, i1)):
                 project_nei(i)
-            for i in not_yet_added:
-                add_to_batch_sums(i)
-            not_yet_added.clear()
             for i in range(i0, i1):
                 square_self_up_to(i)
                 sum_of_squares(h_nei[i], square_sums[i][:, 1:2])
@@ -270,8 +267,9 @@ def tile_batchedgraphsagemean1_b_kernel(
         for i in not_yet_added:
             add_to_batch_sums(i, BLOCKS_OF_SUM_BANK[0])
         first_turned = turn_back(0)
-        for i in not_yet_added:
-            add_to_batch_sums(i, range(len(BLOCKS_OF_SUM_BANK[0]), Q_BLOCKS))
+        for in_bank in BLOCKS_OF_SUM_BANK[1:]:
+            for i in not_yet_added:
+                add_to_batch_sums(i, in_bank)
 
         count_sum_squares = held.tile([P, Q_BLOCKS], F32, name="count_sum_squares")
         minus_var = held.tile([P, Q_BLOCKS], F32, name="minus_var")

@@ -21,11 +21,20 @@ HALF_BLOCKS = F_OUT // P
 COUNT = GRAPHS * NODES
 EPS = 1e-5
 
-PIECE_WIDTHS = ((512, 512), (384, 256, 256, 128))
-WIDEST = 512
+LOOKUP_STEPS = (
+    ((0, 1024, (0, 1, 2, 3)),),
+    (
+        (0, 1024, (0,)),
+        (0, 512, (1, 2, 3)),
+        (512, 256, (1, 2, 3)),
+        (768, 256, (1,)),
+        (768, 128, (2, 3)),
+        (896, 128, (2, 3)),
+    ),
+)
 
+H_BANKS = 4
 AHEAD = 2
-H_BANKS = {"self": 2, "nei": 2}
 
 R_STEP = P + 2
 MOST_IN_BANK = 3
@@ -41,12 +50,12 @@ def tile_batchedgraphsagemean1_b_kernel(
     nc = tc.nc
     with (
         tc.tile_pool(name="held", bufs=1) as held,
-        tc.tile_pool(name="sums", bufs=5 * F_BLOCKS) as sums,
+        tc.tile_pool(name="sums", bufs=2 * F_BLOCKS) as sums,
         tc.tile_pool(name="small", bufs=3 * AHEAD) as small,
         tc.tile_pool(name="scratch", bufs=2) as scratch,
         tc.tile_pool(name="results", bufs=5) as results,
         tc.psum_pool(name="gram_banks", bufs=1) as sum_banks,
-        tc.psum_pool(name="h_banks", bufs=AHEAD) as h_banks,
+        tc.psum_pool(name="h_banks", bufs=H_BANKS) as h_banks,
     ):
         lists = held.tile([P, NEIGHBOURS * NODES // 16], U16, name="lists")
         nc.sync.dma_start(lists[:], offs)
@@ -54,37 +63,34 @@ def tile_batchedgraphsagemean1_b_kernel(
         load_queues = (nc.scalar, nc.sync)
         for a in range(F_BLOCKS):
             load_queues[a % 2].dma_start(x_f32[a][:], x[a * P : (a + 1) * P, :])
-        weights = {}
-        for half_name, w in (("self", w_self), ("nei", w_nei)):
-            weights[half_name] = held.tile([P, F_BLOCKS, F_OUT], BF16, name=f"w_{half_name}")
-            nc.sync.dma_start(weights[half_name][:], w.rearrange("(a p) q -> p a q", p=P))
-        for a in range(F_BLOCKS, GRAPHS * F_BLOCKS):
-            nc.sync.dma_start(x_f32[a][:], x[a * P : (a + 1) * P, :])
-        w_nei_loaded = weights["nei"]
-        weights["nei"] = held.tile([P, F_BLOCKS, F_OUT], BF16, name="w_nei_quarter")
-        nc.scalar.mul(weights["nei"][:], w_nei_loaded[:], 1.0 / NEIGHBOURS)
-
         bias_f32 = held.tile([1, CHANNELS], F32, name="bias_f32")
         nc.scalar.dma_start(bias_f32[:, 0:F_OUT], bias_self.rearrange("q o -> o q"))
         nc.scalar.dma_start(bias_f32[:, F_OUT:CHANNELS], bias_nei.rearrange("q o -> o q"))
+        weights = {}
+        weights["self"] = held.tile([P, F_BLOCKS, F_OUT], BF16, name="w_self")
+        nc.sync.dma_start(weights["self"][:], w_self.rearrange("(a p) q -> p a q", p=P))
+        for a in range(F_BLOCKS, GRAPHS * F_BLOCKS):
+            nc.sync.dma_start(x_f32[a][:], x[a * P : (a + 1) * P, :])
+        w_nei_loaded = held.tile([P, F_BLOCKS, F_OUT], BF16, name="w_nei")
+        nc.sync.dma_start(w_nei_loaded[:], w_nei.rearrange("(a p) q -> p a q", p=P))
         gamma_t = held.tile([P, Q_BLOCKS], F32, name="gamma_t")
         beta_t = held.tile([P, Q_BLOCKS], F32, name="beta_t")
         with nc.allow_non_contiguous_dma(reason="one 4-byte value to a partition, 8 KiB in all"):
             nc.sync.dma_start(gamma_t[:], gamma.rearrange("(j p) o -> p (j o)", p=P))
             nc.sync.dma_start(beta_t[:], beta.rearrange("(j p) o -> p (j o)", p=P))
 
-        zeros = held.tile([P, WIDEST], F32, name="zeros")
+        zeros = held.tile([P, NODES], F32, name="zeros")
         nc.vector.memset(zeros[:], 0.0)
+        first_row = held.tile([P, P], BF16, name="first_row")
+        nc.gpsimd.memset(first_row[:], 0.0)
+        nc.gpsimd.memset(first_row[0:1, :], 1.0)
+        bias_rows = held.tile([P, CHANNELS], BF16, name="bias_rows")
+        nc.gpsimd.memset(bias_rows[:], 0.0)
+        nc.scalar.copy(bias_rows[0:1, :], bias_f32[:])
         ident_bf = held.tile([P, P], BF16, name="ident_bf")
         make_identity(nc, ident_bf[:])
         ident_f32 = held.tile([P, P], F32, name="ident_f32")
         make_identity(nc, ident_f32[:])
-        first_row = held.tile([P, P], BF16, name="first_row")
-        nc.vector.memset(first_row[:], 0.0)
-        nc.vector.memset(first_row[0:1, :], 1.0)
-        bias_rows = held.tile([P, CHANNELS], BF16, name="bias_rows")
-        nc.vector.memset(bias_rows[:], 0.0)
-        nc.scalar.copy(bias_rows[0:1, :], bias_f32[:])
         r_tiles = [
             [held.tile([P, Q_BLOCKS, R_STEP], BF16, name=f"r_{b}_{n}") for n in range(NODE_BLOCKS)]
             for b in range(GRAPHS)
@@ -93,10 +99,8 @@ def tile_batchedgraphsagemean1_b_kernel(
             for n in range(NODE_BLOCKS):
                 nc.vector.memset(r_tiles[b][n][:, :, P : P + 1], 1.0)
 
-        def cut_to_bf16(values, columns):
-            return values.bitcast(BF16)[:, 1 : 2 * columns : 2]
-
-        x_bf = [cut_to_bf16(x_f32[a][:], NODES) for a in range(GRAPHS * F_BLOCKS)]
+        def cut_to_bf16(values, first, columns):
+            return values[:].bitcast(BF16)[:, 2 * first + 1 : 2 * (first + columns) : 2]
 
         sum_tiles = [
             sum_banks.tile([P, MOST_IN_BANK * R_STEP], F32, name=f"gram_{bank}")
@@ -109,16 +113,10 @@ def tile_batchedgraphsagemean1_b_kernel(
             for place, j in enumerate(BLOCKS_OF_SUM_BANK[bank])
         }
 
-        pieces = [
-            (b, sum(PIECE_WIDTHS[b][:earlier]), width)
-            for b in range(GRAPHS)
-            for earlier, width in enumerate(PIECE_WIDTHS[b])
-        ]
-        last_piece_blocks = pieces[-1][2] // P
-        blocks = [(b, n) for b, c0, width in pieces for n in range(c0 // P, (c0 + width) // P)]
+        blocks = [(b, n) for b in range(GRAPHS) for n in range(NODE_BLOCKS)]
 
         def project(half_name, half, nodes_of):
-            h_half = h_banks.tile([P, F_OUT], F32, name=f"h_{half_name}", bufs=H_BANKS[half_name])
+            h_half = h_banks.tile([P, F_OUT], F32, name="h")
             nc.tensor.matmul(
                 h_half[:],
                 lhsT=first_row[:],
@@ -136,32 +134,71 @@ def tile_batchedgraphsagemean1_b_kernel(
                 )
             return h_half
 
+        square_sums = held.tile([P, len(blocks), 2], F32, name="square_sums")
+
         def sum_of_squares(h_half, total):
             squares = scratch.tile([P, F_OUT], BF16, name="squares")
             nc.scalar.activation(squares[:], h_half[:], FUNC.Square, accum_out=total)
 
-        h_self, h_nei, square_sums = {}, {}, {}
-        self_squared = []
+        relu_h_self = []
+        for i, (b, n) in enumerate(blocks):
+            h_self = project(
+                "self", 0, [cut_to_bf16(x_f32[b * F_BLOCKS + f], n * P, P) for f in range(F_BLOCKS)]
+            )
+            sum_of_squares(h_self, square_sums[:, i, 0:1])
+            kept = held.tile([P, F_OUT], F32, name=f"relu_h_self_{i}")
+            nc.scalar.activation(kept[:], h_self[:], FUNC.Relu)
+            relu_h_self.append(kept)
+
+        weights["nei"] = held.tile([P, F_BLOCKS, F_OUT], BF16, name="w_nei_quarter")
+        nc.scalar.mul(weights["nei"][:], w_nei_loaded[:], 1.0 / NEIGHBOURS)
+
+        all_steps = [(b,) + step for b in range(GRAPHS) for step in LOOKUP_STEPS[b]]
+        steps_issued = []
+        sum_of = {}
+        whole = []
+
+        def issue_next_step():
+            b, first_node, nodes, neighbours = all_steps[len(steps_issued)]
+            steps_issued.append(first_node)
+            step_blocks = range(first_node // P, (first_node + nodes) // P)
+            for k in neighbours:
+                first_column = (k * NODES + first_node) // 16
+                offsets = lists[:, first_column : first_column + nodes // 16]
+                for f in range(F_BLOCKS):
+                    so_far, so_far_first = sum_of.get((b, f, first_node // P), (zeros, first_node))
+                    longer = sums.tile([P, nodes], F32, name=f"sum_{nodes}")
+                    nc.vector.tensor_tensor(
+                        longer[:],
+                        x_f32[b * F_BLOCKS + f][:].indirect(offsets),
+                        so_far[:, first_node - so_far_first : first_node - so_far_first + nodes],
+                        ALU.add,
+                    )
+                    for n in step_blocks:
+                        sum_of[b, f, n] = (longer, first_node)
+            if neighbours[-1] == NEIGHBOURS - 1:
+                whole.extend([(b, n) for n in step_blocks])
+
+        h_nei = {}
         not_yet_added = []
 
-        def project_self(i):
+        def project_nei(i):
+            while len(whole) <= i:
+                issue_next_step()
             b, n = blocks[i]
-            in_x = slice(n * P, (n + 1) * P)
-            h_self[i] = project("self", 0, [x_bf[b * F_BLOCKS + f][:, in_x] for f in range(F_BLOCKS)])
-            square_sums[i] = small.tile([P, 2], F32, name="square_sums")
-
-        def square_self_up_to(last):
-            for i in range(len(self_squared), last + 1):
-                sum_of_squares(h_self[i], square_sums[i][:, 0:1])
-                self_squared.append(i)
+            nodes_of = []
+            for f in range(F_BLOCKS):
+                total, total_first = sum_of[b, f, n]
+                nodes_of.append(cut_to_bf16(total, n * P - total_first, P))
+            h_nei[i] = project("nei", 1, nodes_of)
 
         def normalise(i):
             inv_norm = small.tile([P, 1], F32, name="inv_norm")
             nc.scalar.activation(
                 inv_norm[:],
-                square_sums[i][:, 0:1],
+                square_sums[:, i, 0:1],
                 FUNC.Abs_reciprocal_sqrt,
-                bias=square_sums[i][:, 1:2],
+                bias=square_sums[:, i, 1:2],
             )
             b, n = blocks[i]
             r = r_tiles[b][n]
@@ -173,11 +210,11 @@ def tile_batchedgraphsagemean1_b_kernel(
             for j0, j1 in steps:
                 nc.scalar.activation(
                     r[:, j0:j1, 0:P],
-                    h_self[i][:, j0 * P : j1 * P].rearrange("p (j c) -> p j c", c=P),
+                    relu_h_self[i][:, j0 * P : j1 * P].rearrange("p (j c) -> p j c", c=P),
                     FUNC.Relu,
                     scale=inv_norm[:, 0:1],
                 )
-            if i < len(blocks) - last_piece_blocks:
+            if i < len(blocks) - 1:
                 nc.scalar.activation(
                     r[:, HALF_BLOCKS:Q_BLOCKS, 0:P],
                     h_nei[i][:].rearrange("p (j c) -> p j c", c=P),
@@ -207,56 +244,24 @@ def tile_batchedgraphsagemean1_b_kernel(
                     stop=(i == len(blocks) - 1 and j == in_bank[-1]),
                 )
 
-        for i in range(AHEAD):
-            project_self(i)
-        square_self_up_to(AHEAD - 1)
-
-        i1 = 0
-        for t, (b, c0, width) in enumerate(pieces):
-            i0, i1 = i1, i1 + width // P
-            running = [zeros[:, 0:width] for f in range(F_BLOCKS)]
-
-            for k in range(NEIGHBOURS):
-                first_column = (k * NODES + c0) // 16
-                offsets = lists[:, first_column : first_column + width // 16]
-                for f in range(F_BLOCKS):
-                    longer = sums.tile([P, width], F32, name="running_sum")
-                    nc.vector.tensor_tensor(
-                        longer[:], x_f32[b * F_BLOCKS + f][:].indirect(offsets), running[f], ALU.add
-                    )
-                    running[f] = longer[:]
-            agg_bf = [cut_to_bf16(running[f], width) for f in range(F_BLOCKS)]
-
-            def project_nei(i):
-                in_piece = slice((i - i0) * P, (i - i0 + 1) * P)
-                h_nei[i] = project("nei", 1, [agg_bf[f][:, in_piece] for f in range(F_BLOCKS)])
-
-            if t < len(pieces) - 1:
-                for i in not_yet_added:
-                    add_to_batch_sums(i)
-                not_yet_added.clear()
-            for i in range(i0, min(i0 + AHEAD, i1)):
+        for b in range(GRAPHS):
+            i0, i1 = b * NODE_BLOCKS, (b + 1) * NODE_BLOCKS
+            for i in range(i0, i0 + AHEAD):
                 project_nei(i)
             for i in range(i0, i1):
-                square_self_up_to(i)
-                sum_of_squares(h_nei[i], square_sums[i][:, 1:2])
+                sum_of_squares(h_nei[i], square_sums[:, i, 1:2])
                 normalise(i)
-                if i + AHEAD < len(blocks):
-                    project_self(i + AHEAD)
                 if i + AHEAD < i1:
                     project_nei(i + AHEAD)
+                if i + AHEAD < i1 or i1 < len(blocks):
                     add_to_batch_sums(i)
                 else:
                     not_yet_added.append(i)
-            square_self_up_to(min(i1 + AHEAD, len(blocks)) - 1)
 
         def turn_back(j):
             turned = []
             for b in range(GRAPHS):
-                ring = ("nei", "self")[b]
-                r_turned = h_banks.tile(
-                    [P, NODES], BF16, name="r_turned", tag=f"h_{ring}", bufs=H_BANKS[ring]
-                )
+                r_turned = h_banks.tile([P, NODES], BF16, name="r_turned", tag="h")
                 for n in range(NODE_BLOCKS):
                     nc.tensor.transpose(
                         r_turned[:, n * P : (n + 1) * P], r_tiles[b][n][:, j, 0:P], ident_bf[:]

@@ -244,6 +244,17 @@ def tile_batchedgraphsagemean1_b_kernel(
                     stop=(i == len(blocks) - 1 and j == in_bank[-1]),
                 )
 
+        def turn_back(j, turned, some_blocks):
+            for b, n in some_blocks:
+                if n == 0:
+                    turned.append(h_banks.tile([P, NODES], BF16, name="r_turned", tag="h"))
+                nc.tensor.transpose(
+                    turned[b][:, n * P : (n + 1) * P], r_tiles[b][n][:, j, 0:P], ident_bf[:]
+                )
+
+        first_turned = []
+        last = len(blocks) - 1
+        turn_from = last - 2 * AHEAD
         for b in range(GRAPHS):
             i0, i1 = b * NODE_BLOCKS, (b + 1) * NODE_BLOCKS
             for i in range(i0, i0 + AHEAD):
@@ -253,25 +264,16 @@ def tile_batchedgraphsagemean1_b_kernel(
                 normalise(i)
                 if i + AHEAD < i1:
                     project_nei(i + AHEAD)
-                if i + AHEAD < i1 or i1 < len(blocks):
+                if i + AHEAD <= last:
                     add_to_batch_sums(i)
+                    if i >= turn_from:
+                        turn_back(0, first_turned, blocks[0 if i == turn_from else i : i + 1])
                 else:
                     not_yet_added.append(i)
 
-        def turn_back(j):
-            turned = []
-            for b in range(GRAPHS):
-                r_turned = h_banks.tile([P, NODES], BF16, name="r_turned", tag="h")
-                for n in range(NODE_BLOCKS):
-                    nc.tensor.transpose(
-                        r_turned[:, n * P : (n + 1) * P], r_tiles[b][n][:, j, 0:P], ident_bf[:]
-                    )
-                turned.append(r_turned)
-            return turned
-
         for i in not_yet_added:
             add_to_batch_sums(i, BLOCKS_OF_SUM_BANK[0])
-        first_turned = turn_back(0)
+        turn_back(0, first_turned, [blocks[i] for i in not_yet_added])
         for in_bank in BLOCKS_OF_SUM_BANK[1:]:
             for i in not_yet_added:
                 add_to_batch_sums(i, in_bank)
@@ -332,7 +334,10 @@ def tile_batchedgraphsagemean1_b_kernel(
         def write_out(j):
             column = slice(j, j + 1)
             y = results.tile([P, GRAPHS, NODES], F32, name="y")
-            turned = first_turned if j == 0 else turn_back(j)
+            turned = first_turned
+            if j > 0:
+                turned = []
+                turn_back(j, turned, blocks)
             halves = 2 if j == 0 else 1
             for first_node in range(0, NODES, NODES // halves):
                 nodes = slice(first_node, first_node + NODES // halves)

@@ -81,16 +81,16 @@ def tile_batchedgraphsagemean1_b_kernel(
 
         zeros = held.tile([P, NODES], F32, name="zeros")
         nc.vector.memset(zeros[:], 0.0)
+        ident_bf = held.tile([P, P], BF16, name="ident_bf")
+        make_identity(nc, ident_bf[:])
+        ident_f32 = held.tile([P, P], F32, name="ident_f32")
+        make_identity(nc, ident_f32[:])
         first_row = held.tile([P, P], BF16, name="first_row")
         nc.gpsimd.memset(first_row[:], 0.0)
         nc.gpsimd.memset(first_row[0:1, :], 1.0)
         bias_rows = held.tile([P, CHANNELS], BF16, name="bias_rows")
         nc.gpsimd.memset(bias_rows[:], 0.0)
         nc.scalar.copy(bias_rows[0:1, :], bias_f32[:])
-        ident_bf = held.tile([P, P], BF16, name="ident_bf")
-        make_identity(nc, ident_bf[:])
-        ident_f32 = held.tile([P, P], F32, name="ident_f32")
-        make_identity(nc, ident_f32[:])
         r_tiles = [
             [held.tile([P, Q_BLOCKS, R_STEP], BF16, name=f"r_{b}_{n}") for n in range(NODE_BLOCKS)]
             for b in range(GRAPHS)

@@ -333,7 +333,7 @@ def tile_batchedgraphsagemean1_b_kernel(
 
         def write_out(j):
             column = slice(j, j + 1)
-            y = results.tile([P, GRAPHS, NODES], F32, name="y")
+            y = results.tile([P, GRAPHS, NODES], F32, name="y", align_bytes=256)
             turned = first_turned
             if j > 0:
                 turned = []

@@ -97,7 +97,9 @@ def tile_batchedgraphsagemean1_b_kernel(
         ]
         for b in range(GRAPHS):
             for n in range(NODE_BLOCKS):
-                nc.vector.memset(r_tiles[b][n][:, :, P : P + 1], 1.0)
+                nc.vector.memset(r_tiles[b][n][:, :, P : P + 1], 1.0 / COUNT)
+        eps = held.tile([P, 1], F32, name="eps")
+        nc.gpsimd.memset(eps[:], EPS)
 
         def cut_to_bf16(values, first, columns):
             return values[:].bitcast(BF16)[:, 2 * first + 1 : 2 * (first + columns) : 2]
@@ -278,8 +280,8 @@ def tile_batchedgraphsagemean1_b_kernel(
             for i in not_yet_added:
                 add_to_batch_sums(i, in_bank)
 
-        count_sum_squares = held.tile([P, Q_BLOCKS], F32, name="count_sum_squares")
-        minus_var = held.tile([P, Q_BLOCKS], F32, name="minus_var")
+        mean_squared_less_eps = held.tile([P, Q_BLOCKS], F32, name="mean_squared_less_eps")
+        mean_of_squares = held.tile([P, Q_BLOCKS], F32, name="mean_of_squares")
         minus_mean_gamma = held.tile([P, Q_BLOCKS], F32, name="minus_mean_gamma")
         inv_std = held.tile([P, Q_BLOCKS], F32, name="inv_std")
         gain = held.tile([P, Q_BLOCKS], F32, name="gain")
@@ -288,39 +290,39 @@ def tile_batchedgraphsagemean1_b_kernel(
 
         def gain_and_shift(j):
             column = slice(j, j + 1)
-            sum_of_r = batch_sums[j][:, P : P + 1]
+            mean = batch_sums[j][:, P : P + 1]
+            nc.vector.scalar_tensor_tensor(
+                out=mean_squared_less_eps[:, column],
+                in0=mean,
+                scalar=mean,
+                in1=eps[:],
+                op0=ALU.mult,
+                op1=ALU.subtract,
+            )
             diagonal = scratch.tile([P, P], F32, name="diagonal")
             nc.vector.scalar_tensor_tensor(
                 out=diagonal[:],
                 in0=batch_sums[j][:, 0:P],
-                scalar=float(COUNT),
+                scalar=1.0 / COUNT,
                 in1=ident_f32[:],
                 op0=ALU.mult,
                 op1=ALU.mult,
-                accum_out=count_sum_squares[:, column],
-            )
-            nc.vector.scalar_tensor_tensor(
-                out=minus_var[:, column],
-                in0=sum_of_r,
-                scalar=sum_of_r,
-                in1=count_sum_squares[:, column],
-                op0=ALU.mult,
-                op1=ALU.subtract,
+                accum_out=mean_of_squares[:, column],
             )
             nc.vector.scalar_tensor_tensor(
                 out=minus_mean_gamma[:, column],
-                in0=sum_of_r,
-                scalar=-1.0 / COUNT,
+                in0=mean,
+                scalar=-1.0,
                 in1=gamma_t[:, column],
                 op0=ALU.mult,
                 op1=ALU.mult,
             )
             nc.scalar.activation(
                 inv_std[:, column],
-                minus_var[:, column],
+                mean_of_squares[:, column],
                 FUNC.Abs_reciprocal_sqrt,
-                bias=EPS,
-                scale=-1.0 / (COUNT * COUNT),
+                bias=mean_squared_less_eps[:, column],
+                scale=-1.0,
             )
             nc.vector.tensor_tensor(gain[:, column], gamma_t[:, column], inv_std[:, column], ALU.mult)
             nc.scalar.activation(

@@ -27,9 +27,9 @@ LOOKUP_STEPS = (
         (0, 1024, (0,)),
         (0, 512, (1, 2, 3)),
         (512, 256, (1, 2, 3)),
-        (768, 256, (1,)),
-        (768, 128, (2, 3)),
-        (896, 128, (2, 3)),
+        (768, 256, (1, 2)),
+        (768, 128, (3,)),
+        (896, 128, (3,)),
     ),
 )
 
@@ -205,18 +205,18 @@ def tile_batchedgraphsagemean1_b_kernel(
             b, n = blocks[i]
             r = r_tiles[b][n]
             in_first_bank = len(BLOCKS_OF_SUM_BANK[0])
-            if i < len(blocks) - 1:
+            if i < len(blocks) - 2:
                 steps = ((0, HALF_BLOCKS),)
             else:
                 steps = ((0, in_first_bank), (in_first_bank, HALF_BLOCKS))
             for j0, j1 in steps:
-                nc.scalar.activation(
-                    r[:, j0:j1, 0:P],
-                    relu_h_self[i][:, j0 * P : j1 * P].rearrange("p (j c) -> p j c", c=P),
-                    FUNC.Relu,
-                    scale=inv_norm[:, 0:1],
-                )
-            if i < len(blocks) - 1:
+                r_self = r[:, j0:j1, 0:P]
+                kept = relu_h_self[i][:, j0 * P : j1 * P].rearrange("p (j c) -> p j c", c=P)
+                if i == len(blocks) - 2 and j0 > 0:
+                    nc.vector.tensor_scalar(r_self, kept, inv_norm[:, 0:1], 0.0, ALU.mult, ALU.max)
+                else:
+                    nc.scalar.activation(r_self, kept, FUNC.Relu, scale=inv_norm[:, 0:1])
+            if i < len(blocks) - 2:
                 nc.scalar.activation(
                     r[:, HALF_BLOCKS:Q_BLOCKS, 0:P],
                     h_nei[i][:].rearrange("p (j c) -> p j c", c=P),
@@ -264,7 +264,8 @@ def tile_batchedgraphsagemean1_b_kernel(
             for i in range(i0, i1):
                 sum_of_squares(h_nei[i], square_sums[:, i, 1:2])
                 normalise(i)
-                if i + AHEAD < i1:
+                sums_in_front = i + AHEAD == last - 1
+                if i + AHEAD < i1 and not sums_in_front:
                     project_nei(i + AHEAD)
                 if i + AHEAD <= last:
                     add_to_batch_sums(i)
@@ -272,13 +273,15 @@ def tile_batchedgraphsagemean1_b_kernel(
                         turn_back(0, first_turned, blocks[0 if i == turn_from else i : i + 1])
                 else:
                     not_yet_added.append(i)
+                if sums_in_front:
+                    project_nei(i + AHEAD)
 
-        for i in not_yet_added:
-            add_to_batch_sums(i, BLOCKS_OF_SUM_BANK[0])
-        turn_back(0, first_turned, [blocks[i] for i in not_yet_added])
-        for in_bank in BLOCKS_OF_SUM_BANK[1:]:
+        def complete_sum_bank(bank):
             for i in not_yet_added:
-                add_to_batch_sums(i, in_bank)
+                add_to_batch_sums(i, BLOCKS_OF_SUM_BANK[bank])
+
+        complete_sum_bank(0)
+        turn_back(0, first_turned, [blocks[i] for i in not_yet_added])
 
         mean_squared_less_eps = held.tile([P, Q_BLOCKS], F32, name="mean_squared_less_eps")
         mean_of_squares = held.tile([P, Q_BLOCKS], F32, name="mean_of_squares")
@@ -358,5 +361,7 @@ def tile_batchedgraphsagemean1_b_kernel(
         gain_and_shift(0)
         for j in range(Q_BLOCKS):
             if j + 1 < Q_BLOCKS:
+                if j + 1 == BLOCKS_OF_SUM_BANK[sum_bank_of[j + 1]][0]:
+                    complete_sum_bank(sum_bank_of[j + 1])
                 gain_and_shift(j + 1)
             write_out(j)

@@ -212,7 +212,7 @@ def tile_batchedgraphsagemean1_b_kernel(
             for j0, j1 in steps:
                 r_self = r[:, j0:j1, 0:P]
                 kept = relu_h_self[i][:, j0 * P : j1 * P].rearrange("p (j c) -> p j c", c=P)
-                if i == len(blocks) - 2 and j0 > 0:
+                if (i == len(blocks) - 2 and j0 > 0) or (i == len(blocks) - 1 and j0 == 0):
                     nc.vector.tensor_scalar(r_self, kept, inv_norm[:, 0:1], 0.0, ALU.mult, ALU.max)
                 else:
                     nc.scalar.activation(r_self, kept, FUNC.Relu, scale=inv_norm[:, 0:1])

@@ -212,7 +212,7 @@ def tile_batchedgraphsagemean1_b_kernel(
             for j0, j1 in steps:
                 r_self = r[:, j0:j1, 0:P]
                 kept = relu_h_self[i][:, j0 * P : j1 * P].rearrange("p (j c) -> p j c", c=P)
-                if (i == len(blocks) - 2 and j0 > 0) or (i == len(blocks) - 1 and j0 == 0):
+                if i == len(blocks) - 2 or (i == len(blocks) - 1 and j0 == 0):
                     nc.vector.tensor_scalar(r_self, kept, inv_norm[:, 0:1], 0.0, ALU.mult, ALU.max)
                 else:
                     nc.scalar.activation(r_self, kept, FUNC.Relu, scale=inv_norm[:, 0:1])

@@ -204,34 +204,26 @@ def tile_batchedgraphsagemean1_b_kernel(
             )
             b, n = blocks[i]
             r = r_tiles[b][n]
+            self_by_vector = i >= len(blocks) - 2
+            nei_by_vector = i == len(blocks) - 2
             in_first_bank = len(BLOCKS_OF_SUM_BANK[0])
-            if i < len(blocks) - 2:
-                steps = ((0, HALF_BLOCKS),)
-            else:
+            if self_by_vector:
                 steps = ((0, in_first_bank), (in_first_bank, HALF_BLOCKS))
+            else:
+                steps = ((0, HALF_BLOCKS),)
             for j0, j1 in steps:
                 r_self = r[:, j0:j1, 0:P]
                 kept = relu_h_self[i][:, j0 * P : j1 * P].rearrange("p (j c) -> p j c", c=P)
-                if i == len(blocks) - 2 or (i == len(blocks) - 1 and j0 == 0):
+                if self_by_vector:
                     nc.vector.tensor_scalar(r_self, kept, inv_norm[:, 0:1], 0.0, ALU.mult, ALU.max)
                 else:
                     nc.scalar.activation(r_self, kept, FUNC.Relu, scale=inv_norm[:, 0:1])
-            if i < len(blocks) - 2:
-                nc.scalar.activation(
-                    r[:, HALF_BLOCKS:Q_BLOCKS, 0:P],
-                    h_nei[i][:].rearrange("p (j c) -> p j c", c=P),
-                    FUNC.Relu,
-                    scale=inv_norm[:, 0:1],
-                )
+            r_nei = r[:, HALF_BLOCKS:Q_BLOCKS, 0:P]
+            h = h_nei[i][:].rearrange("p (j c) -> p j c", c=P)
+            if nei_by_vector:
+                nc.vector.tensor_scalar(r_nei, h, inv_norm[:, 0:1], 0.0, ALU.mult, ALU.max)
             else:
-                nc.vector.tensor_scalar(
-                    r[:, HALF_BLOCKS:Q_BLOCKS, 0:P],
-                    h_nei[i][:].rearrange("p (j c) -> p j c", c=P),
-                    inv_norm[:, 0:1],
-                    0.0,
-                    ALU.mult,
-                    ALU.max,
-                )
+                nc.scalar.activation(r_nei, h, FUNC.Relu, scale=inv_norm[:, 0:1])
 
         def add_to_batch_sums(i, channel_blocks=range(Q_BLOCKS)):
             b, n = blocks[i]
@@ -328,12 +320,13 @@ def tile_batchedgraphsagemean1_b_kernel(
                 scale=-1.0,
             )
             nc.vector.tensor_tensor(gain[:, column], gamma_t[:, column], inv_std[:, column], ALU.mult)
-            nc.scalar.activation(
-                shift[:, column],
-                minus_mean_gamma[:, column],
-                FUNC.Identity,
-                bias=beta_t[:, column],
-                scale=inv_std[:, column],
+            nc.vector.scalar_tensor_tensor(
+                out=shift[:, column],
+                in0=minus_mean_gamma[:, column],
+                scalar=inv_std[:, column],
+                in1=beta_t[:, column],
+                op0=ALU.mult,
+                op1=ALU.add,
             )
 
         def write_out(j):

@@ -36,7 +36,7 @@ LOOKUP_STEPS = (
 H_BANKS = 4
 AHEAD = 2
 
-R_STEP = P + 2
+R_STEP = P + 8
 MOST_IN_BANK = 3
 BLOCKS_OF_SUM_BANK = ((0,), (1, 2, 3), (4, 5, 6), (7,))
 SUM_BANKS = len(BLOCKS_OF_SUM_BANK)

@@ -50,10 +50,8 @@ def tile_batchedgraphsagemean1_b_kernel(
     nc = tc.nc
     with (
         tc.tile_pool(name="held", bufs=1) as held,
-        tc.tile_pool(name="sums", bufs=2 * F_BLOCKS) as sums,
         tc.tile_pool(name="small", bufs=3 * AHEAD) as small,
         tc.tile_pool(name="scratch", bufs=2) as scratch,
-        tc.tile_pool(name="results", bufs=5) as results,
         tc.psum_pool(name="gram_banks", bufs=1) as sum_banks,
         tc.psum_pool(name="h_banks", bufs=H_BANKS) as h_banks,
     ):
@@ -160,7 +158,7 @@ def tile_batchedgraphsagemean1_b_kernel(
         sum_of = {}
         whole = []
 
-        def issue_next_step():
+        def issue_next_step(sums):
             b, first_node, nodes, neighbours = all_steps[len(steps_issued)]
             steps_issued.append(first_node)
             step_blocks = range(first_node // P, (first_node + nodes) // P)
@@ -184,9 +182,9 @@ def tile_batchedgraphsagemean1_b_kernel(
         h_nei = {}
         not_yet_added = []
 
-        def project_nei(i):
+        def project_nei(sums, i):
             while len(whole) <= i:
-                issue_next_step()
+                issue_next_step(sums)
             b, n = blocks[i]
             nodes_of = []
             for f in range(F_BLOCKS):
@@ -241,32 +239,33 @@ def tile_batchedgraphsagemean1_b_kernel(
         def turn_back(j, turned, some_blocks):
             for b, n in some_blocks:
                 if n == 0:
-                    turned.append(h_banks.tile([P, NODES], BF16, name="r_turned", tag="h"))
+                    turned[b] = h_banks.tile([P, NODES], BF16, name="r_turned", tag="h")
                 nc.tensor.transpose(
                     turned[b][:, n * P : (n + 1) * P], r_tiles[b][n][:, j, 0:P], ident_bf[:]
                 )
 
-        first_turned = []
+        first_turned = {}
         last = len(blocks) - 1
         turn_from = last - 2 * AHEAD
-        for b in range(GRAPHS):
-            i0, i1 = b * NODE_BLOCKS, (b + 1) * NODE_BLOCKS
-            for i in range(i0, i0 + AHEAD):
-                project_nei(i)
-            for i in range(i0, i1):
-                sum_of_squares(h_nei[i], square_sums[:, i, 1:2])
-                normalise(i)
-                sums_in_front = i + AHEAD == last - 1
-                if i + AHEAD < i1 and not sums_in_front:
-                    project_nei(i + AHEAD)
-                if i + AHEAD <= last:
-                    add_to_batch_sums(i)
-                    if i >= turn_from:
-                        turn_back(0, first_turned, blocks[0 if i == turn_from else i : i + 1])
-                else:
-                    not_yet_added.append(i)
-                if sums_in_front:
-                    project_nei(i + AHEAD)
+        with tc.tile_pool(name="sums", bufs=2 * F_BLOCKS) as sums:
+            for b in range(GRAPHS):
+                i0, i1 = b * NODE_BLOCKS, (b + 1) * NODE_BLOCKS
+                for i in range(i0, i0 + AHEAD):
+                    project_nei(sums, i)
+                for i in range(i0, i1):
+                    sum_of_squares(h_nei[i], square_sums[:, i, 1:2])
+                    normalise(i)
+                    sums_in_front = i + AHEAD == last - 1
+                    if i + AHEAD < i1 and not sums_in_front:
+                        project_nei(sums, i + AHEAD)
+                    if i + AHEAD <= last:
+                        add_to_batch_sums(i)
+                        if i >= turn_from:
+                            turn_back(0, first_turned, blocks[0 if i == turn_from else i : i + 1])
+                    else:
+                        not_yet_added.append(i)
+                    if sums_in_front:
+                        project_nei(sums, i + AHEAD)
 
         def complete_sum_bank(bank):
             for i in not_yet_added:
@@ -282,6 +281,7 @@ def tile_batchedgraphsagemean1_b_kernel(
         gain = held.tile([P, Q_BLOCKS], F32, name="gain")
         shift = held.tile([P, Q_BLOCKS], F32, name="shift")
         out_blocks = out.rearrange("(b j p) s -> j p b s", b=GRAPHS, p=P)
+        out_graphs = out.rearrange("(b j p) s -> b p j s", b=GRAPHS, p=P)
 
         def gain_and_shift(j):
             column = slice(j, j + 1)
@@ -329,32 +329,52 @@ def tile_batchedgraphsagemean1_b_kernel(
                 op1=ALU.add,
             )
 
-        def write_out(j):
+        def scale_and_shift(j, by_scalar, y_part, turned_part):
             column = slice(j, j + 1)
+            if by_scalar:
+                nc.scalar.activation(
+                    y_part, turned_part, FUNC.Identity, bias=shift[:, column], scale=gain[:, column]
+                )
+            else:
+                nc.vector.tensor_scalar(
+                    y_part, turned_part, gain[:, column], shift[:, column], ALU.mult, ALU.add
+                )
+
+        def statistics(j):
+            if j > 0 and j == BLOCKS_OF_SUM_BANK[sum_bank_of[j]][0]:
+                complete_sum_bank(sum_bank_of[j])
+            gain_and_shift(j)
+
+        def write_out_block(results, j):
             y = results.tile([P, GRAPHS, NODES], F32, name="y", align_bytes=256)
             turned = first_turned
             if j > 0:
-                turned = []
+                turned = {}
                 turn_back(j, turned, blocks)
             halves = 2 if j == 0 else 1
             for first_node in range(0, NODES, NODES // halves):
                 nodes = slice(first_node, first_node + NODES // halves)
-                nc.scalar.activation(
-                    y[:, 0, nodes],
-                    turned[0][:, nodes],
-                    FUNC.Identity,
-                    bias=shift[:, column],
-                    scale=gain[:, column],
-                )
-                nc.vector.tensor_scalar(
-                    y[:, 1, nodes], turned[1][:, nodes], gain[:, column], shift[:, column], ALU.mult, ALU.add
-                )
+                for b in range(GRAPHS):
+                    scale_and_shift(j, b == 0, y[:, b, nodes], turned[b][:, nodes])
                 nc.sync.dma_start(out_blocks[j][:, :, nodes], y[:, :, nodes])
 
-        gain_and_shift(0)
-        for j in range(Q_BLOCKS):
-            if j + 1 < Q_BLOCKS:
-                if j + 1 == BLOCKS_OF_SUM_BANK[sum_bank_of[j + 1]][0]:
-                    complete_sum_bank(sum_bank_of[j + 1])
-                gain_and_shift(j + 1)
-            write_out(j)
+        def write_out_nei_half(wide_results, b):
+            y = wide_results.tile([P, HALF_BLOCKS, NODES], F32, name="y_wide", align_bytes=256)
+            for j in range(HALF_BLOCKS, Q_BLOCKS):
+                if b == 0 and j + 1 < Q_BLOCKS:
+                    statistics(j + 1)
+                turned = {}
+                turn_back(j, turned, blocks[b * NODE_BLOCKS : (b + 1) * NODE_BLOCKS])
+                scale_and_shift(j, j % 2 == 0, y[:, j - HALF_BLOCKS, :], turned[b][:])
+            nc.sync.dma_start(out_graphs[b][:, HALF_BLOCKS:Q_BLOCKS, :], y[:])
+
+        with (
+            tc.tile_pool(name="results", bufs=HALF_BLOCKS) as results,
+            tc.tile_pool(name="wide_results", bufs=GRAPHS) as wide_results,
+        ):
+            statistics(0)
+            for j in range(HALF_BLOCKS):
+                statistics(j + 1)
+                write_out_block(results, j)
+            for b in range(GRAPHS):
+                write_out_nei_half(wide_results, b)

@@ -240,8 +240,12 @@ def tile_batchedgraphsagemean1_b_kernel(
             for b, n in some_blocks:
                 if n == 0:
                     turned[b] = h_banks.tile([P, NODES], BF16, name="r_turned", tag="h")
-                nc.tensor.transpose(
-                    turned[b][:, n * P : (n + 1) * P], r_tiles[b][n][:, j, 0:P], ident_bf[:]
+                nc.tensor.matmul(
+                    turned[b][:, n * P : (n + 1) * P],
+                    lhsT=r_tiles[b][n][:, j, 0:P],
+                    rhs=ident_bf[:],
+                    start=True,
+                    stop=True,
                 )
 
         first_turned = {}

@@ -73,9 +73,12 @@ def tile_batchedgraphsagemean1_b_kernel(
         nc.sync.dma_start(w_nei_loaded[:], w_nei.rearrange("(a p) q -> p a q", p=P))
         gamma_t = held.tile([P, Q_BLOCKS], F32, name="gamma_t")
         beta_t = held.tile([P, Q_BLOCKS], F32, name="beta_t")
-        with nc.allow_non_contiguous_dma(reason="one 4-byte value to a partition, 8 KiB in all"):
-            nc.sync.dma_start(gamma_t[:], gamma.rearrange("(j p) o -> p (j o)", p=P))
-            nc.sync.dma_start(beta_t[:], beta.rearrange("(j p) o -> p (j o)", p=P))
+        with nc.allow_non_contiguous_dma(reason="pieces of 16 bytes, 8 KiB in all"):
+            for loaded, vector in ((gamma_t, gamma), (beta_t, beta)):
+                nc.sync.dma_start(
+                    loaded[:].rearrange("p (t e) -> p t e", e=HALF_BLOCKS),
+                    vector.rearrange("(t p e) o -> p t (e o)", p=P, e=HALF_BLOCKS),
+                )
 
         zeros = held.tile([P, NODES], F32, name="zeros")
         nc.vector.memset(zeros[:], 0.0)
@@ -192,6 +195,9 @@ def tile_batchedgraphsagemean1_b_kernel(
                 nodes_of.append(cut_to_bf16(total, n * P - total_first, P))
             h_nei[i] = project("nei", 1, nodes_of)
 
+        def in_order_of_h(channel_blocks):
+            return channel_blocks.rearrange("p e c -> p c e")
+
         def normalise(i):
             inv_norm = small.tile([P, 1], F32, name="inv_norm")
             nc.scalar.activation(
@@ -210,14 +216,14 @@ def tile_batchedgraphsagemean1_b_kernel(
             else:
                 steps = ((0, HALF_BLOCKS),)
             for j0, j1 in steps:
-                r_self = r[:, j0:j1, 0:P]
-                kept = relu_h_self[i][:, j0 * P : j1 * P].rearrange("p (j c) -> p j c", c=P)
+                r_self = in_order_of_h(r[:, j0:j1, 0:P])
+                kept = relu_h_self[i][:].rearrange("p (c e) -> p c e", e=HALF_BLOCKS)[:, :, j0:j1]
                 if self_by_vector:
                     nc.vector.tensor_scalar(r_self, kept, inv_norm[:, 0:1], 0.0, ALU.mult, ALU.max)
                 else:
                     nc.scalar.activation(r_self, kept, FUNC.Relu, scale=inv_norm[:, 0:1])
-            r_nei = r[:, HALF_BLOCKS:Q_BLOCKS, 0:P]
-            h = h_nei[i][:].rearrange("p (j c) -> p j c", c=P)
+            r_nei = in_order_of_h(r[:, HALF_BLOCKS:Q_BLOCKS, 0:P])
+            h = h_nei[i][:].rearrange("p (c e) -> p c e", e=HALF_BLOCKS)
             if nei_by_vector:
                 nc.vector.tensor_scalar(r_nei, h, inv_norm[:, 0:1], 0.0, ALU.mult, ALU.max)
             else:
@@ -284,8 +290,8 @@ def tile_batchedgraphsagemean1_b_kernel(
         inv_std = held.tile([P, Q_BLOCKS], F32, name="inv_std")
         gain = held.tile([P, Q_BLOCKS], F32, name="gain")
         shift = held.tile([P, Q_BLOCKS], F32, name="shift")
-        out_blocks = out.rearrange("(b j p) s -> j p b s", b=GRAPHS, p=P)
-        out_graphs = out.rearrange("(b j p) s -> b p j s", b=GRAPHS, p=P)
+        out_blocks = out.rearrange("(b t p e) s -> t e p b s", b=GRAPHS, p=P, e=HALF_BLOCKS)
+        out_runs = out.rearrange("(b t p e) s -> b p t (e s)", b=GRAPHS, p=P, e=HALF_BLOCKS)
 
         def gain_and_shift(j):
             column = slice(j, j + 1)
@@ -349,8 +355,7 @@ def tile_batchedgraphsagemean1_b_kernel(
                 complete_sum_bank(sum_bank_of[j])
             gain_and_shift(j)
 
-        def write_out_block(results, j):
-            y = results.tile([P, GRAPHS, NODES], F32, name="y", align_bytes=256)
+        def write_out_block(y, j):
             turned = first_turned
             if j > 0:
                 turned = {}
@@ -360,25 +365,36 @@ def tile_batchedgraphsagemean1_b_kernel(
                 nodes = slice(first_node, first_node + NODES // halves)
                 for b in range(GRAPHS):
                     scale_and_shift(j, b == 0, y[:, b, nodes], turned[b][:, nodes])
-                nc.sync.dma_start(out_blocks[j][:, :, nodes], y[:, :, nodes])
+                nc.sync.dma_start(
+                    out_blocks[j // HALF_BLOCKS][j % HALF_BLOCKS][:, :, nodes], y[:, :, nodes]
+                )
 
-        def write_out_nei_half(wide_results, b):
-            y = wide_results.tile([P, HALF_BLOCKS, NODES], F32, name="y_wide", align_bytes=256)
-            for j in range(HALF_BLOCKS, Q_BLOCKS):
+        def write_out_run(y, b, j0, j1):
+            for j in range(j0, j1):
                 if b == 0 and j + 1 < Q_BLOCKS:
                     statistics(j + 1)
                 turned = {}
                 turn_back(j, turned, blocks[b * NODE_BLOCKS : (b + 1) * NODE_BLOCKS])
-                scale_and_shift(j, j % 2 == 0, y[:, j - HALF_BLOCKS, :], turned[b][:])
-            nc.sync.dma_start(out_graphs[b][:, HALF_BLOCKS:Q_BLOCKS, :], y[:])
+                scale_and_shift(j, j % 2 == 0, y[:, j - j0, :], turned[b][:])
+            e0 = j0 % HALF_BLOCKS
+            nc.sync.dma_start(
+                out_runs[b][:, j0 // HALF_BLOCKS, e0 * NODES : (e0 + j1 - j0) * NODES],
+                y[:].rearrange("p e s -> p (e s)"),
+            )
 
+        alone = 2
         with (
-            tc.tile_pool(name="results", bufs=HALF_BLOCKS) as results,
+            tc.tile_pool(name="results", bufs=alone + GRAPHS) as results,
             tc.tile_pool(name="wide_results", bufs=GRAPHS) as wide_results,
         ):
             statistics(0)
-            for j in range(HALF_BLOCKS):
+            for j in range(alone):
                 statistics(j + 1)
-                write_out_block(results, j)
+                y = results.tile([P, GRAPHS, NODES], F32, name="y", align_bytes=256)
+                write_out_block(y, j)
             for b in range(GRAPHS):
-                write_out_nei_half(wide_results, b)
+                y = results.tile([P, HALF_BLOCKS - alone, NODES], F32, name="y", align_bytes=256)
+                write_out_run(y, b, alone, HALF_BLOCKS)
+            for b in range(GRAPHS):
+                y_wide = wide_results.tile([P, HALF_BLOCKS, NODES], F32, name="y_wide", align_bytes=256)
+                write_out_run(y_wide, b, HALF_BLOCKS, Q_BLOCKS)

@@ -291,7 +291,7 @@ def tile_batchedgraphsagemean1_b_kernel(
         gain = held.tile([P, Q_BLOCKS], F32, name="gain")
         shift = held.tile([P, Q_BLOCKS], F32, name="shift")
         out_blocks = out.rearrange("(b t p e) s -> t e p b s", b=GRAPHS, p=P, e=HALF_BLOCKS)
-        out_runs = out.rearrange("(b t p e) s -> b p t (e s)", b=GRAPHS, p=P, e=HALF_BLOCKS)
+        out_runs = out.rearrange("(b t p e) s -> p b t (e s)", b=GRAPHS, p=P, e=HALF_BLOCKS)
 
         def gain_and_shift(j):
             column = slice(j, j + 1)
@@ -369,32 +369,39 @@ def tile_batchedgraphsagemean1_b_kernel(
                     out_blocks[j // HALF_BLOCKS][j % HALF_BLOCKS][:, :, nodes], y[:, :, nodes]
                 )
 
-        def write_out_run(y, b, j0, j1):
-            for j in range(j0, j1):
-                if b == 0 and j + 1 < Q_BLOCKS:
-                    statistics(j + 1)
-                turned = {}
-                turn_back(j, turned, blocks[b * NODE_BLOCKS : (b + 1) * NODE_BLOCKS])
-                scale_and_shift(j, j % 2 == 0, y[:, j - j0, :], turned[b][:])
+        def write_out_run(y, graphs, j0, j1):
+            for b in graphs:
+                for j in range(j0, j1):
+                    if b == 0 and j + 1 < Q_BLOCKS:
+                        statistics(j + 1)
+                    turned = {}
+                    turn_back(j, turned, blocks[b * NODE_BLOCKS : (b + 1) * NODE_BLOCKS])
+                    scale_and_shift(j, j % 2 == 0, y[:, b - graphs[0], j - j0, :], turned[b][:])
             e0 = j0 % HALF_BLOCKS
             nc.sync.dma_start(
-                out_runs[b][:, j0 // HALF_BLOCKS, e0 * NODES : (e0 + j1 - j0) * NODES],
-                y[:].rearrange("p e s -> p (e s)"),
+                out_runs[
+                    :,
+                    graphs[0] : graphs[-1] + 1,
+                    j0 // HALF_BLOCKS,
+                    e0 * NODES : (e0 + j1 - j0) * NODES,
+                ],
+                y[:].rearrange("p b e s -> p b (e s)"),
             )
 
         alone = 2
+        pair = 2
         with (
-            tc.tile_pool(name="results", bufs=alone + GRAPHS) as results,
-            tc.tile_pool(name="wide_results", bufs=GRAPHS) as wide_results,
+            tc.tile_pool(name="results", bufs=alone + 2 * GRAPHS) as results,
+            tc.tile_pool(name="last_results", bufs=1) as last_results,
         ):
             statistics(0)
             for j in range(alone):
                 statistics(j + 1)
                 y = results.tile([P, GRAPHS, NODES], F32, name="y", align_bytes=256)
                 write_out_block(y, j)
-            for b in range(GRAPHS):
-                y = results.tile([P, HALF_BLOCKS - alone, NODES], F32, name="y", align_bytes=256)
-                write_out_run(y, b, alone, HALF_BLOCKS)
-            for b in range(GRAPHS):
-                y_wide = wide_results.tile([P, HALF_BLOCKS, NODES], F32, name="y_wide", align_bytes=256)
-                write_out_run(y_wide, b, HALF_BLOCKS, Q_BLOCKS)
+            for j0 in range(alone, Q_BLOCKS - pair, pair):
+                for b in range(GRAPHS):
+                    y = results.tile([P, 1, pair, NODES], F32, name="y", align_bytes=256)
+                    write_out_run(y, (b,), j0, j0 + pair)
+            y_last = last_results.tile([P, GRAPHS, pair, NODES], F32, name="y_last", align_bytes=256)
+            write_out_run(y_last, (0, 1), Q_BLOCKS - pair, Q_BLOCKS)

@@ -156,6 +156,12 @@ def tile_batchedgraphsagemean1_b_kernel(
         weights["nei"] = held.tile([P, F_BLOCKS, F_OUT], BF16, name="w_nei_quarter")
         nc.scalar.mul(weights["nei"][:], w_nei_loaded[:], 1.0 / NEIGHBOURS)
 
+        factors = held.tile([P, Q_BLOCKS, 2], F32, name="factors")
+        nc.scalar.copy(factors[:, :, 0:1], gamma_t[:].unsqueeze(2))
+        addends = held.tile([P, Q_BLOCKS, 2], F32, name="addends")
+        nc.gpsimd.memset(addends[:], 0.0)
+        nc.scalar.copy(addends[:, :, 1:2], beta_t[:].unsqueeze(2))
+
         all_steps = [(b,) + step for b in range(GRAPHS) for step in LOOKUP_STEPS[b]]
         steps_issued = []
         sum_of = {}
@@ -286,10 +292,8 @@ def tile_batchedgraphsagemean1_b_kernel(
 
         mean_squared_less_eps = held.tile([P, Q_BLOCKS], F32, name="mean_squared_less_eps")
         mean_of_squares = held.tile([P, Q_BLOCKS], F32, name="mean_of_squares")
-        minus_mean_gamma = held.tile([P, Q_BLOCKS], F32, name="minus_mean_gamma")
         inv_std = held.tile([P, Q_BLOCKS], F32, name="inv_std")
-        gain = held.tile([P, Q_BLOCKS], F32, name="gain")
-        shift = held.tile([P, Q_BLOCKS], F32, name="shift")
+        gain_shift = held.tile([P, Q_BLOCKS, 2], F32, name="gain_shift")
         out_blocks = out.rearrange("(b t p e) s -> t e p b s", b=GRAPHS, p=P, e=HALF_BLOCKS)
         out_runs = out.rearrange("(b t p e) s -> p b t (e s)", b=GRAPHS, p=P, e=HALF_BLOCKS)
 
@@ -315,7 +319,7 @@ def tile_batchedgraphsagemean1_b_kernel(
                 accum_out=mean_of_squares[:, column],
             )
             nc.vector.scalar_tensor_tensor(
-                out=minus_mean_gamma[:, column],
+                out=factors[:, j, 1:2],
                 in0=mean,
                 scalar=-1.0,
                 in1=gamma_t[:, column],
@@ -329,26 +333,21 @@ def tile_batchedgraphsagemean1_b_kernel(
                 bias=mean_squared_less_eps[:, column],
                 scale=-1.0,
             )
-            nc.vector.tensor_tensor(gain[:, column], gamma_t[:, column], inv_std[:, column], ALU.mult)
             nc.vector.scalar_tensor_tensor(
-                out=shift[:, column],
-                in0=minus_mean_gamma[:, column],
+                out=gain_shift[:, j, :],
+                in0=factors[:, j, :],
                 scalar=inv_std[:, column],
-                in1=beta_t[:, column],
+                in1=addends[:, j, :],
                 op0=ALU.mult,
                 op1=ALU.add,
             )
 
         def scale_and_shift(j, by_scalar, y_part, turned_part):
-            column = slice(j, j + 1)
+            gain, shift = gain_shift[:, j, 0:1], gain_shift[:, j, 1:2]
             if by_scalar:
-                nc.scalar.activation(
-                    y_part, turned_part, FUNC.Identity, bias=shift[:, column], scale=gain[:, column]
-                )
+                nc.scalar.activation(y_part, turned_part, FUNC.Identity, bias=shift, scale=gain)
             else:
-                nc.vector.tensor_scalar(
-                    y_part, turned_part, gain[:, column], shift[:, column], ALU.mult, ALU.add
-                )
+                nc.vector.tensor_scalar(y_part, turned_part, gain, shift, ALU.mult, ALU.add)
 
         def statistics(j):
             if j > 0 and j == BLOCKS_OF_SUM_BANK[sum_bank_of[j]][0]:

@@ -143,14 +143,21 @@ def tile_batchedgraphsagemean1_b_kernel(
             squares = scratch.tile([P, F_OUT], BF16, name="squares")
             nc.scalar.activation(squares[:], h_half[:], FUNC.Square, accum_out=total)
 
+        def in_order_of_h(channel_blocks):
+            return channel_blocks.rearrange("p e c -> p c e")
+
         relu_h_self = []
         for i, (b, n) in enumerate(blocks):
             h_self = project(
                 "self", 0, [cut_to_bf16(x_f32[b * F_BLOCKS + f], n * P, P) for f in range(F_BLOCKS)]
             )
             sum_of_squares(h_self, square_sums[:, i, 0:1])
-            kept = held.tile([P, F_OUT], F32, name=f"relu_h_self_{i}")
-            nc.scalar.activation(kept[:], h_self[:], FUNC.Relu)
+            kept = held.tile([P, HALF_BLOCKS, P], F32, name=f"relu_h_self_{i}")
+            nc.scalar.activation(
+                in_order_of_h(kept[:]),
+                h_self[:].rearrange("p (c e) -> p c e", e=HALF_BLOCKS),
+                FUNC.Relu,
+            )
             relu_h_self.append(kept)
 
         weights["nei"] = held.tile([P, F_BLOCKS, F_OUT], BF16, name="w_nei_quarter")
@@ -201,9 +208,6 @@ def tile_batchedgraphsagemean1_b_kernel(
                 nodes_of.append(cut_to_bf16(total, n * P - total_first, P))
             h_nei[i] = project("nei", 1, nodes_of)
 
-        def in_order_of_h(channel_blocks):
-            return channel_blocks.rearrange("p e c -> p c e")
-
         def normalise(i):
             inv_norm = small.tile([P, 1], F32, name="inv_norm")
             nc.scalar.activation(
@@ -222,8 +226,8 @@ def tile_batchedgraphsagemean1_b_kernel(
             else:
                 steps = ((0, HALF_BLOCKS),)
             for j0, j1 in steps:
-                r_self = in_order_of_h(r[:, j0:j1, 0:P])
-                kept = relu_h_self[i][:].rearrange("p (c e) -> p c e", e=HALF_BLOCKS)[:, :, j0:j1]
+                r_self = r[:, j0:j1, 0:P]
+                kept = relu_h_self[i][:, j0:j1, :]
                 if self_by_vector:
                     nc.vector.tensor_scalar(r_self, kept, inv_norm[:, 0:1], 0.0, ALU.mult, ALU.max)
                 else:

import concourse.mybir as mybir
from concourse.masks import make_identity

F32 = mybir.dt.float32
BF16 = mybir.dt.bfloat16
U16 = mybir.dt.uint16
FUNC = mybir.ActivationFunctionType
ALU = mybir.AluOpType

P = 128
GRAPHS = 2
NODES = 1024
NEIGHBOURS = 4
F_IN = 512
F_OUT = 512
CHANNELS = 2 * F_OUT
F_BLOCKS = F_IN // P
Q_BLOCKS = CHANNELS // P
NODE_BLOCKS = NODES // P
HALF_BLOCKS = F_OUT // P
COUNT = GRAPHS * NODES
EPS = 1e-5

LOOKUP_STEPS = (
    ((0, 1024, (0, 1, 2, 3)),),
    (
        (0, 1024, (0,)),
        (0, 512, (1, 2, 3)),
        (512, 256, (1, 2, 3)),
        (768, 256, (1, 2)),
        (768, 128, (3,)),
        (896, 128, (3,)),
    ),
)

H_BANKS = 4
AHEAD = 2

R_STEP = P + 8
MOST_IN_BANK = 3
BLOCKS_OF_SUM_BANK = ((0,), (1, 2, 3), (4, 5, 6), (7,))
SUM_BANKS = len(BLOCKS_OF_SUM_BANK)

FLOPS = 2 * GRAPHS * NODES * F_IN * CHANNELS


def tile_batchedgraphsagemean1_b_kernel(
    tc, x, w_self, bias_self, w_nei, bias_nei, gamma, beta, offs, out
):
    nc = tc.nc
    with (
        tc.tile_pool(name="held", bufs=1) as held,
        tc.tile_pool(name="small", bufs=3 * AHEAD) as small,
        tc.tile_pool(name="scratch", bufs=2) as scratch,
        tc.psum_pool(name="gram_banks", bufs=1) as sum_banks,
        tc.psum_pool(name="h_banks", bufs=H_BANKS) as h_banks,
    ):
        lists = held.tile([P, NEIGHBOURS * NODES // 16], U16, name="lists")
        nc.sync.dma_start(lists[:], offs)
        x_f32 = [held.tile([P, NODES], F32, name=f"x_f32_{a}") for a in range(GRAPHS * F_BLOCKS)]
        load_queues = (nc.scalar, nc.sync)
        for a in range(F_BLOCKS):
            load_queues[a % 2].dma_start(x_f32[a][:], x[a * P : (a + 1) * P, :])
        bias_f32 = held.tile([1, CHANNELS], F32, name="bias_f32")
        nc.scalar.dma_start(bias_f32[:, 0:F_OUT], bias_self.rearrange("q o -> o q"))
        nc.scalar.dma_start(bias_f32[:, F_OUT:CHANNELS], bias_nei.rearrange("q o -> o q"))
        weights = {}
        weights["self"] = held.tile([P, F_BLOCKS, F_OUT], BF16, name="w_self")
        nc.sync.dma_start(weights["self"][:], w_self.rearrange("(a p) q -> p a q", p=P))
        for a in range(F_BLOCKS, GRAPHS * F_BLOCKS):
            nc.sync.dma_start(x_f32[a][:], x[a * P : (a + 1) * P, :])
        w_nei_loaded = held.tile([P, F_BLOCKS, F_OUT], BF16, name="w_nei")
        nc.sync.dma_start(w_nei_loaded[:], w_nei.rearrange("(a p) q -> p a q", p=P))
        gamma_t = held.tile([P, Q_BLOCKS], F32, name="gamma_t")
        beta_t = held.tile([P, Q_BLOCKS], F32, name="beta_t")
        with nc.allow_non_contiguous_dma(reason="pieces of 16 bytes, 8 KiB in all"):
            for loaded, vector in ((gamma_t, gamma), (beta_t, beta)):
                nc.sync.dma_start(
                    loaded[:].rearrange("p (t e) -> p t e", e=HALF_BLOCKS),
                    vector.rearrange("(t p e) o -> p t (e o)", p=P, e=HALF_BLOCKS),
                )

        zeros = held.tile([P, NODES], F32, name="zeros")
        nc.vector.memset(zeros[:], 0.0)
        ident_bf = held.tile([P, P], BF16, name="ident_bf")
        make_identity(nc, ident_bf[:])
        ident_f32 = held.tile([P, P], F32, name="ident_f32")
        make_identity(nc, ident_f32[:])
        first_row = held.tile([P, P], BF16, name="first_row")
        nc.gpsimd.memset(first_row[:], 0.0)
        nc.gpsimd.memset(first_row[0:1, :], 1.0)
        bias_rows = held.tile([P, CHANNELS], BF16, name="bias_rows")
        nc.gpsimd.memset(bias_rows[:], 0.0)
        nc.scalar.copy(bias_rows[0:1, :], bias_f32[:])
        r_tiles = [
            [held.tile([P, Q_BLOCKS, R_STEP], BF16, name=f"r_{b}_{n}") for n in range(NODE_BLOCKS)]
            for b in range(GRAPHS)
        ]
        for b in range(GRAPHS):
            for n in range(NODE_BLOCKS):
                nc.vector.memset(r_tiles[b][n][:, :, P : P + 1], 1.0 / COUNT)
        eps = held.tile([P, 1], F32, name="eps")
        nc.gpsimd.memset(eps[:], EPS)

        def cut_to_bf16(values, first, columns):
            return values[:].bitcast(BF16)[:, 2 * first + 1 : 2 * (first + columns) : 2]

        sum_tiles = [
            sum_banks.tile([P, MOST_IN_BANK * R_STEP], F32, name=f"gram_{bank}")
            for bank in range(SUM_BANKS)
        ]
        sum_bank_of = {j: bank for bank in range(SUM_BANKS) for j in BLOCKS_OF_SUM_BANK[bank]}
        batch_sums = {
            j: sum_tiles[bank][:, place * R_STEP : place * R_STEP + P + 1]
            for bank in range(SUM_BANKS)
            for place, j in enumerate(BLOCKS_OF_SUM_BANK[bank])
        }

        blocks = [(b, n) for b in range(GRAPHS) for n in range(NODE_BLOCKS)]

        def project(half_name, half, nodes_of):
            h_half = h_banks.tile([P, F_OUT], F32, name="h")
            nc.tensor.matmul(
                h_half[:],
                lhsT=first_row[:],
                rhs=bias_rows[:, half * F_OUT : (half + 1) * F_OUT],
                start=True,
                stop=False,
            )
            for f in range(F_BLOCKS):
                nc.tensor.matmul(
                    h_half[:],
                    lhsT=nodes_of[f],
                    rhs=weights[half_name][:, f, :],
                    start=False,
                    stop=(f == F_BLOCKS - 1),
                )
            return h_half

        square_sums = held.tile([P, len(blocks), 2], F32, name="square_sums")

        def sum_of_squares(h_half, total):
            squares = scratch.tile([P, F_OUT], BF16, name="squares")
            nc.scalar.activation(squares[:], h_half[:], FUNC.Square, accum_out=total)

        def in_order_of_h(channel_blocks):
            return channel_blocks.rearrange("p e c -> p c e")

        relu_h_self = []
        for i, (b, n) in enumerate(blocks):
            h_self = project(
                "self", 0, [cut_to_bf16(x_f32[b * F_BLOCKS + f], n * P, P) for f in range(F_BLOCKS)]
            )
            sum_of_squares(h_self, square_sums[:, i, 0:1])
            kept = held.tile([P, HALF_BLOCKS, P], F32, name=f"relu_h_self_{i}")
            nc.scalar.activation(
                in_order_of_h(kept[:]),
                h_self[:].rearrange("p (c e) -> p c e", e=HALF_BLOCKS),
                FUNC.Relu,
            )
            relu_h_self.append(kept)

        weights["nei"] = held.tile([P, F_BLOCKS, F_OUT], BF16, name="w_nei_quarter")
        nc.scalar.mul(weights["nei"][:], w_nei_loaded[:], 1.0 / NEIGHBOURS)

        factors = held.tile([P, Q_BLOCKS, 2], F32, name="factors")
        nc.scalar.copy(factors[:, :, 0:1], gamma_t[:].unsqueeze(2))
        addends = held.tile([P, Q_BLOCKS, 2], F32, name="addends")
        nc.gpsimd.memset(addends[:], 0.0)
        nc.scalar.copy(addends[:, :, 1:2], beta_t[:].unsqueeze(2))

        all_steps = [(b,) + step for b in range(GRAPHS) for step in LOOKUP_STEPS[b]]
        steps_issued = []
        sum_of = {}
        whole = []

        def issue_next_step(sums):
            b, first_node, nodes, neighbours = all_steps[len(steps_issued)]
            steps_issued.append(first_node)
            step_blocks = range(first_node // P, (first_node + nodes) // P)
            for k in neighbours:
                first_column = (k * NODES + first_node) // 16
                offsets = lists[:, first_column : first_column + nodes // 16]
                for f in range(F_BLOCKS):
                    so_far, so_far_first = sum_of.get((b, f, first_node // P), (zeros, first_node))
                    longer = sums.tile([P, nodes], F32, name=f"sum_{nodes}")
                    nc.vector.tensor_tensor(
                        longer[:],
                        x_f32[b * F_BLOCKS + f][:].indirect(offsets),
                        so_far[:, first_node - so_far_first : first_node - so_far_first + nodes],
                        ALU.add,
                    )
                    for n in step_blocks:
                        sum_of[b, f, n] = (longer, first_node)
            if neighbours[-1] == NEIGHBOURS - 1:
                whole.extend([(b, n) for n in step_blocks])

        h_nei = {}
        not_yet_added = []

        def project_nei(sums, i):
            while len(whole) <= i:
                issue_next_step(sums)
            b, n = blocks[i]
            nodes_of = []
            for f in range(F_BLOCKS):
                total, total_first = sum_of[b, f, n]
                nodes_of.append(cut_to_bf16(total, n * P - total_first, P))
            h_nei[i] = project("nei", 1, nodes_of)

        def normalise(i):
            inv_norm = small.tile([P, 1], F32, name="inv_norm")
            nc.scalar.activation(
                inv_norm[:],
                square_sums[:, i, 0:1],
                FUNC.Abs_reciprocal_sqrt,
                bias=square_sums[:, i, 1:2],
            )
            b, n = blocks[i]
            r = r_tiles[b][n]
            self_by_vector = i >= len(blocks) - 2
            nei_by_vector = i == len(blocks) - 2
            in_first_bank = len(BLOCKS_OF_SUM_BANK[0])
            if self_by_vector:
                steps = ((0, in_first_bank), (in_first_bank, HALF_BLOCKS))
            else:
                steps = ((0, HALF_BLOCKS),)
            for j0, j1 in steps:
                r_self = r[:, j0:j1, 0:P]
                kept = relu_h_self[i][:, j0:j1, :]
                if self_by_vector:
                    nc.vector.tensor_scalar(r_self, kept, inv_norm[:, 0:1], 0.0, ALU.mult, ALU.max)
                else:
                    nc.scalar.activation(r_self, kept, FUNC.Relu, scale=inv_norm[:, 0:1])
            r_nei = in_order_of_h(r[:, HALF_BLOCKS:Q_BLOCKS, 0:P])
            h = h_nei[i][:].rearrange("p (c e) -> p c e", e=HALF_BLOCKS)
            if nei_by_vector:
                nc.vector.tensor_scalar(r_nei, h, inv_norm[:, 0:1], 0.0, ALU.mult, ALU.max)
            else:
                nc.scalar.activation(r_nei, h, FUNC.Relu, scale=inv_norm[:, 0:1])

        def add_to_batch_sums(i, channel_blocks=range(Q_BLOCKS)):
            b, n = blocks[i]
            r = r_tiles[b][n]
            for j in channel_blocks:
                in_bank = BLOCKS_OF_SUM_BANK[sum_bank_of[j]]
                nc.tensor.matmul(
                    batch_sums[j],
                    lhsT=r[:, j, 0:P],
                    rhs=r[:, j, 0 : P + 1],
                    start=(i == 0 and j == in_bank[0]),
                    stop=(i == len(blocks) - 1 and j == in_bank[-1]),
                )

        def turn_back(j, turned, some_blocks):
            for b, n in some_blocks:
                if n == 0:
                    turned[b] = h_banks.tile([P, NODES], BF16, name="r_turned", tag="h")
                nc.tensor.matmul(
                    turned[b][:, n * P : (n + 1) * P],
                    lhsT=r_tiles[b][n][:, j, 0:P],
                    rhs=ident_bf[:],
                    start=True,
                    stop=True,
                )

        first_turned = {}
        last = len(blocks) - 1
        turn_from = last - 2 * AHEAD
        with tc.tile_pool(name="sums", bufs=2 * F_BLOCKS) as sums:
            for b in range(GRAPHS):
                i0, i1 = b * NODE_BLOCKS, (b + 1) * NODE_BLOCKS
                for i in range(i0, i0 + AHEAD):
                    project_nei(sums, i)
                for i in range(i0, i1):
                    sum_of_squares(h_nei[i], square_sums[:, i, 1:2])
                    normalise(i)
                    sums_in_front = i + AHEAD == last - 1
                    if i + AHEAD < i1 and not sums_in_front:
                        project_nei(sums, i + AHEAD)
                    if i + AHEAD <= last:
                        add_to_batch_sums(i)
                        if i >= turn_from:
                            turn_back(0, first_turned, blocks[0 if i == turn_from else i : i + 1])
                    else:
                        not_yet_added.append(i)
                    if sums_in_front:
                        project_nei(sums, i + AHEAD)

        def complete_sum_bank(bank):
            for i in not_yet_added:
                add_to_batch_sums(i, BLOCKS_OF_SUM_BANK[bank])

        complete_sum_bank(0)
        turn_back(0, first_turned, [blocks[i] for i in not_yet_added])

        mean_squared_less_eps = held.tile([P, Q_BLOCKS], F32, name="mean_squared_less_eps")
        mean_of_squares = held.tile([P, Q_BLOCKS], F32, name="mean_of_squares")
        inv_std = held.tile([P, Q_BLOCKS], F32, name="inv_std")
        gain_shift = held.tile([P, Q_BLOCKS, 2], F32, name="gain_shift")
        out_blocks = out.rearrange("(b t p e) s -> t e p b s", b=GRAPHS, p=P, e=HALF_BLOCKS)
        out_runs = out.rearrange("(b t p e) s -> p b t (e s)", b=GRAPHS, p=P, e=HALF_BLOCKS)

        def gain_and_shift(j):
            column = slice(j, j + 1)
            mean = batch_sums[j][:, P : P + 1]
            nc.vector.scalar_tensor_tensor(
                out=mean_squared_less_eps[:, column],
                in0=mean,
                scalar=mean,
                in1=eps[:],
                op0=ALU.mult,
                op1=ALU.subtract,
            )
            diagonal = scratch.tile([P, P], F32, name="diagonal")
            nc.vector.scalar_tensor_tensor(
                out=diagonal[:],
                in0=batch_sums[j][:, 0:P],
                scalar=1.0 / COUNT,
                in1=ident_f32[:],
                op0=ALU.mult,
                op1=ALU.mult,
                accum_out=mean_of_squares[:, column],
            )
            nc.vector.scalar_tensor_tensor(
                out=factors[:, j, 1:2],
                in0=mean,
                scalar=-1.0,
                in1=gamma_t[:, column],
                op0=ALU.mult,
                op1=ALU.mult,
            )
            nc.scalar.activation(
                inv_std[:, column],
                mean_of_squares[:, column],
                FUNC.Abs_reciprocal_sqrt,
                bias=mean_squared_less_eps[:, column],
                scale=-1.0,
            )
            nc.vector.scalar_tensor_tensor(
                out=gain_shift[:, j, :],
                in0=factors[:, j, :],
                scalar=inv_std[:, column],
                in1=addends[:, j, :],
                op0=ALU.mult,
                op1=ALU.add,
            )

        def scale_and_shift(j, by_scalar, y_part, turned_part):
            gain, shift = gain_shift[:, j, 0:1], gain_shift[:, j, 1:2]
            if by_scalar:
                nc.scalar.activation(y_part, turned_part, FUNC.Identity, bias=shift, scale=gain)
            else:
                nc.vector.tensor_scalar(y_part, turned_part, gain, shift, ALU.mult, ALU.add)

        def statistics(j):
            if j > 0 and j == BLOCKS_OF_SUM_BANK[sum_bank_of[j]][0]:
                complete_sum_bank(sum_bank_of[j])
            gain_and_shift(j)

        def write_out_block(y, j):
            turned = first_turned
            if j > 0:
                turned = {}
                turn_back(j, turned, blocks)
            halves = 2 if j == 0 else 1
            for first_node in range(0, NODES, NODES // halves):
                nodes = slice(first_node, first_node + NODES // halves)
                for b in range(GRAPHS):
                    scale_and_shift(j, b == 0, y[:, b, nodes], turned[b][:, nodes])
                nc.sync.dma_start(
                    out_blocks[j // HALF_BLOCKS][j % HALF_BLOCKS][:, :, nodes], y[:, :, nodes]
                )

        def write_out_run(y, graphs, j0, j1):
            for b in graphs:
                for j in range(j0, j1):
                    if b == 0 and j + 1 < Q_BLOCKS:
                        statistics(j + 1)
                    turned = {}
                    turn_back(j, turned, blocks[b * NODE_BLOCKS : (b + 1) * NODE_BLOCKS])
                    scale_and_shift(j, j % 2 == 0, y[:, b - graphs[0], j - j0, :], turned[b][:])
            e0 = j0 % HALF_BLOCKS
            nc.sync.dma_start(
                out_runs[
                    :,
                    graphs[0] : graphs[-1] + 1,
                    j0 // HALF_BLOCKS,
                    e0 * NODES : (e0 + j1 - j0) * NODES,
                ],
                y[:].rearrange("p b e s -> p b (e s)"),
            )

        alone = 2
        pair = 2
        with (
            tc.tile_pool(name="results", bufs=alone + 2 * GRAPHS) as results,
            tc.tile_pool(name="last_results", bufs=1) as last_results,
        ):
            statistics(0)
            for j in range(alone):
                statistics(j + 1)
                y = results.tile([P, GRAPHS, NODES], F32, name="y", align_bytes=256)
                write_out_block(y, j)
            for j0 in range(alone, Q_BLOCKS - pair, pair):
                for b in range(GRAPHS):
                    y = results.tile([P, 1, pair, NODES], F32, name="y", align_bytes=256)
                    write_out_run(y, (b,), j0, j0 + pair)
            y_last = last_results.tile([P, GRAPHS, pair, NODES], F32, name="y_last", align_bytes=256)
            write_out_run(y_last, (0, 1), Q_BLOCKS - pair, Q_BLOCKS)
